import numpy as np
import ml_dtypes


def mxq(x, axis, fmt="e4m3"):
    dtype, down = {"e4m3": (ml_dtypes.float8_e4m3fn, 7), "e5m2": (ml_dtypes.float8_e5m2, 14)}[fmt]
    v = np.moveaxis(np.asarray(x, np.float32).astype(ml_dtypes.bfloat16).astype(np.float64), axis, -1)
    blocks = v.reshape(v.shape[:-1] + (-1, 32))
    amax = np.abs(blocks).max(-1, keepdims=True)
    byte = np.maximum(np.where(amax > 0, np.frexp(amax)[1] - 1 + 127, 0) - down, 1)
    scale = np.exp2(byte - 127.0)
    codes = (blocks / scale).astype(np.float32).astype(dtype).astype(np.float64)
    return np.moveaxis((codes * scale).reshape(v.shape), -1, axis)


WIDE = False


def mx_kscale(k):
    if not WIDE:
        return np.ones(k)
    levels = np.array([10, -10, 5, -5, 0])
    a = np.random.permutation(np.resize(levels, k // 512 * 4)).reshape(k // 512, 4)
    idx = np.arange(k)
    return np.exp2(a[idx // 512, idx % 128 // 32])


BF16 = ml_dtypes.bfloat16


def bf(x):
    return np.asarray(x, np.float32).astype(BF16)


def f64(x):
    return np.asarray(x).astype(np.float64)


E2M1 = np.array([0.0, 0.5, 1.0, 1.5, 2.0, 3.0, 4.0, 6.0, -0.0, -0.5, -1.0, -1.5, -2.0, -3.0, -4.0, -6.0])


def pack_weight(w, fmt):
    k, n = w.shape
    w = f64(bf(w)).reshape(k // 32, 32, n)
    amax = np.abs(w).max(1)
    if fmt == "e4m3":
        byte = np.frexp(amax)[1] - 1 + 127 - 7
    else:
        mant, ex = np.frexp(amax / 6.0)
        byte = np.where(mant > 0.5, ex, ex - 1) + 127
    byte = np.clip(np.where(amax > 0, byte, 1), 1, 254)
    scaled = (w * np.exp2(127.0 - byte)[:, None, :]).reshape(k, n).astype(np.float32)
    by_word = np.ascontiguousarray(scaled.reshape(k // 512, 128, 4, n).transpose(0, 1, 3, 2))
    if fmt == "e4m3":
        words = by_word.astype(ml_dtypes.float8_e4m3fn).view(np.uint8)
    else:
        c = by_word.astype(ml_dtypes.float4_e2m1fn).view(np.uint8) & 0xF
        words = c[..., 0::2] | (c[..., 1::2] << 4)
    return np.ascontiguousarray(words), np.ascontiguousarray(byte.astype(np.uint8).reshape(k // 512, 16, n))


def unpack_weight(words, scales, fmt):
    g, p, n, _ = words.shape
    if fmt == "e4m3":
        vals = np.ascontiguousarray(words).view(ml_dtypes.float8_e4m3fn).astype(np.float64)
    else:
        nib = np.empty((g, p, n, 4), np.uint8)
        nib[..., 0::2] = words & 0xF
        nib[..., 1::2] = words >> 4
        vals = E2M1[nib]
    vals = vals * np.repeat(np.exp2(scales.astype(np.float64) - 127.0), 8, axis=1)[..., None]
    return vals.transpose(0, 1, 3, 2).reshape(g * 512, n)


B, PED, NED, CED = 1536, 320, 128, 512
Q = PED // 4
FEAT = 2 * PED + 3 * NED


def leaky(v):
    return np.where(v >= 0.0, v, 0.01 * v)


def point_enc(xy, wsx, bsx, wcx, bcx, wsy, bsy, wcy, bcy):
    x = xy[:, 0:1]
    y = xy[:, 1:2]
    return np.concatenate([np.sin(x * wsx + bsx), np.cos(x * wcx + bcx), np.sin(y * wsy + bsy), np.cos(y * wcy + bcy)], axis=-1)


def num_enc(t, w, b):
    return leaky(t[:, None] * w + b)


def setup_inputs():
    s = np.array(mx_kscale(FEAT), dtype=np.float64)
    s[:2 * PED] = 1.0
    t = mx_kscale(CED)
    d = {'src_xy': bf(np.random.standard_normal((B, 2))), 'dst_xy': bf(np.random.standard_normal((B, 2))),
         'time_s': bf(np.random.uniform(size=B)), 'wait_src': bf(np.random.uniform(size=B)), 'wait_dst': bf(np.random.uniform(size=B))}
    for pfx in ('src', 'dst'):
        for part in ('wsx', 'bsx', 'wcx', 'bcx', 'wsy', 'bsy', 'wcy', 'bcy'):
            d[pfx + '_' + part] = bf(np.random.standard_normal(Q) * (1.0 if part[0] == 'w' else 0.1))
    for i, pfx in enumerate(('t', 'ws', 'wd')):
        sn = s[2 * PED + i * NED:2 * PED + (i + 1) * NED]
        d[pfx + '_w'] = bf(np.random.standard_normal(NED) * sn)
        d[pfx + '_b'] = bf(np.random.standard_normal(NED) * 0.1 * sn)
    d['W1_words'], d['W1_scales'] = pack_weight(np.random.standard_normal((FEAT, CED)) * 1.5 / np.sqrt(FEAT) / s[:, None] * t[None, :], 'e4m3')
    d['b1'] = bf(np.random.standard_normal(CED) * 0.1 * t)
    d['W2_words'], d['W2_scales'] = pack_weight(np.random.standard_normal((CED, CED)) * 1.5 / np.sqrt(CED) / t[:, None], 'e4m3')
    d['b2'] = bf(np.random.standard_normal(CED) * 0.1)
    return d


def reference(src_xy, dst_xy, time_s, wait_src, wait_dst,
              src_wsx, src_bsx, src_wcx, src_bcx, src_wsy, src_bsy, src_wcy, src_bcy,
              dst_wsx, dst_bsx, dst_wcx, dst_bcx, dst_wsy, dst_bsy, dst_wcy, dst_bcy,
              t_w, t_b, ws_w, ws_b, wd_w, wd_b,
              W1_words, W1_scales, b1, W2_words, W2_scales, b2):
    feats = np.concatenate([
        point_enc(f64(src_xy), f64(src_wsx), f64(src_bsx), f64(src_wcx), f64(src_bcx),
                        f64(src_wsy), f64(src_bsy), f64(src_wcy), f64(src_bcy)),
        point_enc(f64(dst_xy), f64(dst_wsx), f64(dst_bsx), f64(dst_wcx), f64(dst_bcx),
                        f64(dst_wsy), f64(dst_bsy), f64(dst_wcy), f64(dst_bcy)),
        num_enc(f64(time_s), f64(t_w), f64(t_b)),
        num_enc(f64(wait_src), f64(ws_w), f64(ws_b)),
        num_enc(f64(wait_dst), f64(wd_w), f64(wd_b)),
    ], axis=-1)
    h = leaky((mxq(feats, 1, 'e4m3') @ unpack_weight(W1_words, W1_scales, 'e4m3')) + f64(b1))
    return leaky((mxq(h, 1, 'e4m3') @ unpack_weight(W2_words, W2_scales, 'e4m3')) + f64(b2))

@@ -1,0 +1,359 @@
+import math
+from contextlib import ExitStack
+
+import concourse.mybir as mybir
+from concourse.masks import make_identity
+
+F32 = mybir.dt.float32
+BF16 = mybir.dt.bfloat16
+I32 = mybir.dt.int32
+U32 = mybir.dt.uint32
+U8 = mybir.dt.uint8
+FP8X4 = mybir.dt.float8_e4m3fn_x4
+ACT = mybir.ActivationFunctionType
+ALU = mybir.AluOpType
+
+P = 128
+PACK = 4
+K_PASS = P * PACK
+CLAIMS = 1536
+CHUNK = 512
+N_CHUNKS = CLAIMS // CHUNK
+QUARTER = 80
+POINT_FEATURES = 8 * QUARTER
+NUMBER_WIDTH = 128
+HIDDEN = 512
+OUT_WIDTH = 512
+TAIL = POINT_FEATURES - K_PASS
+TAIL_PARTITIONS = TAIL // PACK
+SLOPE = 0.01
+TURN = 2.0 * math.pi
+
+ROW_PHASE = 0
+ROW_W = 1
+ROW_B = 2
+N_ROWS = 3
+
+FLOPS = 2 * CLAIMS * (2 * K_PASS * HIDDEN + HIDDEN * OUT_WIDTH)
+
+
+def tile_claimencoder_kernel(
+    tc,
+    src_xy, dst_xy, time_s, wait_src, wait_dst,
+    src_wsx, src_bsx, src_wcx, src_bcx, src_wsy, src_bsy, src_wcy, src_bcy,
+    dst_wsx, dst_bsx, dst_wcx, dst_bcx, dst_wsy, dst_bsy, dst_wcy, dst_bcy,
+    t_w, t_b, ws_w, ws_b, wd_w, wd_b,
+    W1_words, W1_scales, b1, W2_words, W2_scales, b2,
+    out,
+):
+    nc = tc.nc
+    with ExitStack() as stack:
+        keep = stack.enter_context(tc.tile_pool(name="keep", bufs=1))
+        stack.enter_context(tc.manual_schedule())
+        work = stack.enter_context(tc.tile_pool(name="work", bufs=3))
+        stream = stack.enter_context(tc.tile_pool(name="stream", bufs=4))
+        psum_x = stack.enter_context(tc.psum_pool(name="psum_x", bufs=2))
+        psum_t = stack.enter_context(tc.psum_pool(name="psum_t", bufs=1))
+        psum_h = stack.enter_context(tc.psum_pool(name="psum_h", bufs=2))
+        psum_o = stack.enter_context(tc.psum_pool(name="psum_o", bufs=3))
+
+        ident = keep.tile([P, P], BF16)
+        number_rows = keep.tile([P, CLAIMS], BF16)
+        point_rows = keep.tile([P, 2 * CLAIMS], BF16)
+        number_vecs = keep.tile([P, K_PASS], BF16)
+        head_vecs = keep.tile([P, K_PASS], BF16)
+        tail_vecs = keep.tile([P, K_PASS], BF16)
+        b1_rows = keep.tile([P, P], BF16)
+        SEL_X, SEL_Y, SEL_NUMBER, SEL_TAIL = 0, 1, 2, 3
+        sel = keep.tile([P, SEL_TAIL + N_CHUNKS, P], BF16)
+
+        w1_words = keep.tile([P, 2, HIDDEN], U32, align_bytes=64)
+        w1_scales = keep.tile([P, 2, HIDDEN], U8, align_bytes=64)
+        w1_tail_words = keep.tile([P, N_CHUNKS, HIDDEN], U32, align_bytes=64)
+        w1_tail_scales = keep.tile([P, N_CHUNKS, HIDDEN], U8, align_bytes=64)
+        w2_words = keep.tile([P, OUT_WIDTH], U32, align_bytes=64)
+        w2_scales = keep.tile([P, OUT_WIDTH], U8, align_bytes=64)
+        b2_all = keep.tile([P, OUT_WIDTH], BF16)
+
+        make_identity(nc, ident[:])
+        nc.gpsimd.dma_start(out=b2_all[:], in_=b2.partition_broadcast(P))
+        nc.gpsimd.memset(w1_scales[:].bitcast(F32), 0.0)
+        nc.gpsimd.memset(w1_tail_scales[:].bitcast(F32), 0.0)
+        nc.gpsimd.memset(w1_tail_words[:].bitcast(F32), 0.0)
+        nc.gpsimd.memset(w2_scales[:].bitcast(F32), 0.0)
+        warm = keep.tile([P, 1], F32)
+        nc.vector.memset(warm[:], 0.0)
+        nc.scalar.activation(out=warm[:], in_=warm[:], func=ACT.Sin)
+        nc.vector.memset(number_rows[:], 0.0)
+        nc.vector.memset(number_vecs[:], 0.0)
+        nc.vector.memset(b1_rows[:], 0.0)
+        nc.vector.memset(sel[:], 0.0)
+        for r in range(3):
+            nc.vector.memset(sel[32 * r : 32 * r + 1, SEL_NUMBER, 32 * (r + 1) : 32 * (r + 2)], 1.0)
+        nc.vector.memset(point_rows[:], 0.0)
+        nc.vector.memset(head_vecs[:], 0.0)
+        nc.vector.memset(tail_vecs[:], 0.0)
+        half = 2 * QUARTER // PACK
+        nc.vector.memset(sel[0:1, SEL_X, 0:half], 1.0)
+        nc.vector.memset(sel[0:1, SEL_Y, half : 2 * half], 1.0)
+        nc.vector.memset(sel[32:33, SEL_X, 2 * half : 3 * half], 1.0)
+        nc.vector.memset(sel[32:33, SEL_Y, 3 * half : P], 1.0)
+        for i in range(N_CHUNKS):
+            quadrant = slice(TAIL_PARTITIONS * i, TAIL_PARTITIONS * (i + 1))
+            nc.vector.memset(sel[32:33, SEL_TAIL + i, quadrant], 1.0)
+
+        def load_row(queue, rows, row, first, vector):
+            width = vector.shape[0]
+            queue.dma_start(out=rows[row : row + 1, first : first + width], in_=vector.unsqueeze(0))
+
+        for r, numbers in enumerate((time_s, wait_src, wait_dst)):
+            load_row(nc.sync, number_rows, 32 * r, 0, numbers)
+        for r, (w, b) in enumerate(((t_w, t_b), (ws_w, ws_b), (wd_w, wd_b))):
+            first = TAIL + NUMBER_WIDTH * r
+            load_row(nc.sync, number_vecs, ROW_W, first, w)
+            load_row(nc.sync, number_vecs, ROW_B, first, b)
+
+        nc.sync.dma_start(out=b1_rows[0 : HIDDEN // P, :], in_=b1.rearrange("(mt m) -> mt m", m=P))
+        load_row(nc.sync, point_rows, 32, 0, dst_xy.rearrange("c two -> (c two)"))
+        load_row(nc.sync, point_rows, 0, 0, src_xy.rearrange("c two -> (c two)"))
+
+        def load_point_vector(queue, row, vector, first):
+            head = max(0, min(QUARTER, K_PASS - first))
+            if head > 0:
+                load_row(queue, head_vecs, row, first, vector[0:head])
+            if head < QUARTER:
+                rest = QUARTER - head
+                at = first + head - K_PASS
+                copies = tail_vecs[row : row + 1, 0 : N_CHUNKS * TAIL].rearrange("o (i k) -> o i k", k=TAIL)
+                queue.dma_start(
+                    out=copies[:, :, at : at + rest],
+                    in_=vector[head:QUARTER].unsqueeze(0).unsqueeze(0).to_broadcast([1, N_CHUNKS, rest]),
+                )
+
+        point_parts = (
+            (src_wsx, src_bsx), (src_wcx, src_bcx), (src_wsy, src_bsy), (src_wcy, src_bcy),
+            (dst_wsx, dst_bsx), (dst_wcx, dst_bcx), (dst_wsy, dst_bsy), (dst_wcy, dst_bcy),
+        )
+        for q in reversed(range(len(point_parts))):
+            w, b = point_parts[q]
+            first = QUARTER * q
+            load_point_vector(nc.sync, ROW_W, w, first)
+            load_point_vector(nc.sync, ROW_B, b, first)
+            if q % 2 == 1:
+                head = max(0, min(QUARTER, K_PASS - first))
+                if head > 0:
+                    nc.vector.memset(head_vecs[ROW_PHASE : ROW_PHASE + 1, first : first + head], 0.25)
+                for i in range(N_CHUNKS):
+                    if head < QUARTER:
+                        at = TAIL * i + first + head - K_PASS
+                        nc.vector.memset(tail_vecs[ROW_PHASE : ROW_PHASE + 1, at : at + QUARTER - head], 0.25)
+
+        nc.sync.dma_start(
+            out=w1_words[:].bitcast(I32),
+            in_=W1_words.rearrange("g p n t -> p g (n t)").bitcast(I32),
+        )
+        for quad in range(4):
+            nc.sync.dma_start(
+                out=w1_scales[32 * quad : 32 * quad + 4, :, :].bitcast(I32),
+                in_=W1_scales[:, 4 * quad : 4 * quad + 4, :].rearrange("g r n -> r g n").bitcast(I32),
+            )
+        for i in range(N_CHUNKS):
+            base = TAIL_PARTITIONS * i
+            nc.sync.dma_start(
+                out=w1_tail_words[base : base + TAIL_PARTITIONS, i, :].bitcast(I32),
+                in_=W1_words[1, 0:TAIL_PARTITIONS].rearrange("p n t -> p (n t)").bitcast(I32),
+            )
+            nc.sync.dma_start(
+                out=w1_tail_scales[base : base + 4, i, :].bitcast(I32),
+                in_=W1_scales[1, 0:4, :].bitcast(I32),
+            )
+        nc.sync.dma_start(
+            out=w2_words[:].bitcast(I32),
+            in_=W2_words[0].rearrange("p n t -> p (n t)").bitcast(I32),
+        )
+        for quad in range(4):
+            nc.sync.dma_start(
+                out=w2_scales[32 * quad : 32 * quad + 4, :].bitcast(I32),
+                in_=W2_scales[0, 4 * quad : 4 * quad + 4, :].bitcast(I32),
+            )
+
+        vecs_of = {"number": number_vecs, "head": head_vecs, "tail": tail_vecs}
+        params_of = {}
+
+        def prepare(kind):
+            if kind in params_of:
+                return
+            turned = psum_t.tile([P, PACK, P], BF16, tag="turned")
+            for t in range(PACK):
+                nc.tensor.transpose(turned[:, t, :], vecs_of[kind][:, t : K_PASS : PACK], ident[:])
+            params = keep.tile([P, PACK, N_ROWS], F32, name="params_" + kind)
+            nc.vector.tensor_copy(out=params[:], in_=turned[:, :, 0:N_ROWS])
+            if kind != "number":
+                nc.vector.tensor_scalar_mul(
+                    out=params[:, :, ROW_W : ROW_B + 1], in0=params[:, :, ROW_W : ROW_B + 1], scalar1=1.0 / TURN
+                )
+                nc.vector.tensor_add(
+                    out=params[:, :, ROW_B : ROW_B + 1],
+                    in0=params[:, :, ROW_B : ROW_B + 1],
+                    in1=params[:, :, ROW_PHASE : ROW_PHASE + 1],
+                )
+            params_of[kind] = params
+
+        xy = point_rows[:].rearrange("p (c two) -> p c two", two=2)
+        x_of = {}
+        lines_of = {}
+        grouped_of = {}
+        codes_of = {}
+        scales_of = {}
+
+        def spread_claims(unit):
+            kind, i = unit
+            claims = slice(CHUNK * i, CHUNK * (i + 1))
+            x = psum_x.tile([P, CHUNK], F32)
+            if kind == "number":
+                nc.tensor.matmul(x[:], lhsT=sel[:, SEL_NUMBER, :], rhs=number_rows[:, claims], start=True, stop=True)
+            if kind == "head":
+                nc.tensor.matmul(x[:], lhsT=sel[:, SEL_X, :], rhs=xy[:, claims, 0], start=True, stop=False)
+                nc.tensor.matmul(x[:], lhsT=sel[:, SEL_Y, :], rhs=xy[:, claims, 1], start=False, stop=True)
+            if kind == "tail":
+                for j in range(N_CHUNKS):
+                    nc.tensor.matmul(
+                        x[:], lhsT=sel[:, SEL_TAIL + j, :], rhs=xy[:, CHUNK * j : CHUNK * (j + 1), 1],
+                        start=(j == 0), stop=(j == N_CHUNKS - 1),
+                    )
+            x_of[unit] = x
+
+        def make_lines(unit):
+            x = x_of[unit]
+            params = params_of[unit[0]]
+            lines = work.tile([P, PACK, CHUNK], F32)
+            for t in range(PACK):
+                nc.scalar.activation(
+                    out=lines[:, t, :],
+                    in_=x[:],
+                    func=ACT.Identity,
+                    scale=params[:, t, ROW_W : ROW_W + 1],
+                    bias=params[:, t, ROW_B : ROW_B + 1],
+                )
+            lines_of[unit] = lines
+
+        def leaky_grouped(lines, grouped):
+            by_claim = lines[:].rearrange("p t c -> p c t")
+            nc.vector.scalar_tensor_tensor(
+                out=grouped[:], in0=by_claim, scalar=SLOPE, in1=by_claim, op0=ALU.mult, op1=ALU.max
+            )
+
+        def finish(unit):
+            lines = lines_of[unit]
+            grouped = work.tile([P, CHUNK, PACK], BF16, align_bytes=64)
+            if unit[0] == "number":
+                leaky_grouped(lines, grouped)
+            else:
+                whole = work.tile([P, PACK, CHUNK], I32)
+                nc.vector.tensor_copy(out=whole[:], in_=lines[:])
+                nc.vector.tensor_tensor(out=lines[:], in0=lines[:], in1=whole[:], op=ALU.subtract)
+                nc.scalar.activation(
+                    out=grouped[:], in_=lines[:].rearrange("p t c -> p c t"), func=ACT.Sin, scale=TURN
+                )
+            grouped_of[unit] = grouped
+
+        def quantise(grouped, name):
+            codes = keep.tile([P, CHUNK], U32, align_bytes=64, name="codes_" + name)
+            scales = keep.tile([P, CHUNK], U8, align_bytes=64, name="scales_" + name)
+            nc.vector.quantize_mx(
+                out=codes[:].bitcast(FP8X4), scales=scales[:], in_=grouped[:].rearrange("p c t -> p (c t)")
+            )
+            return codes, scales
+
+        def layer1(i):
+            passes = (
+                (w1_words[:, 0, :], w1_scales[:, 0, :], ("head", i)),
+                (w1_words[:, 1, :], w1_scales[:, 1, :], ("number", i)),
+                (w1_tail_words[:, i, :], w1_tail_scales[:, i, :], ("tail", 0)),
+            )
+            for mt in range(HIDDEN // P):
+                units = slice(P * mt, P * (mt + 1))
+                acc = psum_h.tile([P, CHUNK], F32)
+                for n, (words, scales, unit) in enumerate(passes):
+                    nc.tensor.matmul_mx(
+                        out=acc[:],
+                        lhsT=words[:, units].bitcast(FP8X4),
+                        lhsT_scale=scales[:, units],
+                        rhs=codes_of[unit][:].bitcast(FP8X4),
+                        rhs_scale=scales_of[unit][:],
+                        start=(n == 0),
+                        stop=(n == len(passes) - 1),
+                    )
+                biased = stream.tile([P, CHUNK], F32)
+                nc.scalar.activation(
+                    out=biased[:], in_=acc[:], func=ACT.Identity, bias=b1_cols[:, mt : mt + 1], scale=1.0
+                )
+                first = CHUNK * i + P * mt
+                nc.sync.dma_start(out=out[first : first + P, :], in_=biased[:])
+            parked = work.tile([P, PACK, CHUNK], F32)
+            nc.sync.dma_start(
+                out=parked[:], in_=out[CHUNK * i : CHUNK * (i + 1), :].rearrange("(p t) c -> p t c", t=PACK)
+            )
+            lines_of[("hidden", i)] = parked
+
+        def finish_hidden(i):
+            h = work.tile([P, CHUNK, PACK], BF16, align_bytes=64)
+            leaky_grouped(lines_of[("hidden", i)], h)
+            grouped_of[("hidden", i)] = h
+
+        def layer2(i, codes, scales):
+            for j in range(CHUNK // P):
+                claims = slice(P * j, P * (j + 1))
+                acc = psum_o.tile([P, OUT_WIDTH], F32)
+                nc.tensor.matmul_mx(
+                    out=acc[:],
+                    lhsT=codes[:, claims].bitcast(FP8X4),
+                    lhsT_scale=scales[:, claims],
+                    rhs=w2_words[:].bitcast(FP8X4),
+                    rhs_scale=w2_scales[:],
+                    start=True,
+                    stop=True,
+                )
+                z = stream.tile([P, OUT_WIDTH], F32)
+                nc.vector.tensor_tensor(out=z[:], in0=acc[:], in1=b2_all[:], op=ALU.add)
+                result = stream.tile([P, OUT_WIDTH], F32)
+                nc.vector.scalar_tensor_tensor(
+                    out=result[:], in0=z[:], scalar=SLOPE, in1=z[:], op0=ALU.mult, op1=ALU.max
+                )
+                first = CHUNK * i + P * j
+                nc.sync.dma_start(out=out[first : first + P, :], in_=result[:])
+
+        def second_half(i):
+            finish_hidden(i)
+            codes, scales = quantise(grouped_of[("hidden", i)], "hidden%d" % i)
+            layer2(i, codes, scales)
+
+        units = []
+        for i in range(N_CHUNKS):
+            units.append(("number", i))
+            if i == 0:
+                units.append(("tail", 0))
+            units.append(("head", i))
+        prepare(units[0][0])
+        b1_turned = psum_t.tile([P, P], BF16, tag="turned")
+        nc.tensor.transpose(b1_turned[:], b1_rows[:], ident[:])
+        b1_cols = keep.tile([P, HIDDEN // P], F32)
+        nc.vector.tensor_copy(out=b1_cols[:], in_=b1_turned[:, 0 : HIDDEN // P])
+        spread_claims(units[0])
+        for u in range(len(units) + 2):
+            if u + 1 < len(units):
+                spread_claims(units[u + 1])
+            if u < len(units):
+                make_lines(units[u])
+            if 0 <= u - 1 < len(units):
+                finish(units[u - 1])
+            if u >= 2:
+                unit = units[u - 2]
+                codes_of[unit], scales_of[unit] = quantise(grouped_of[unit], "%s%d" % unit)
+                if unit[0] == "head":
+                    layer1(unit[1])
+                    if unit[1] > 0:
+                        second_half(unit[1] - 1)
+            if u + 1 < len(units):
+                prepare(units[u + 1][0])
+        second_half(N_CHUNKS - 1)

@@ -51,20 +51,20 @@ def tile_claimencoder_kernel(
         keep = stack.enter_context(tc.tile_pool(name="keep", bufs=1))
         stack.enter_context(tc.manual_schedule())
         work = stack.enter_context(tc.tile_pool(name="work", bufs=3))
+        pair = stack.enter_context(tc.tile_pool(name="pair", bufs=2))
         stream = stack.enter_context(tc.tile_pool(name="stream", bufs=4))
         psum_x = stack.enter_context(tc.psum_pool(name="psum_x", bufs=2))
-        psum_t = stack.enter_context(tc.psum_pool(name="psum_t", bufs=1))
-        psum_h = stack.enter_context(tc.psum_pool(name="psum_h", bufs=2))
-        psum_o = stack.enter_context(tc.psum_pool(name="psum_o", bufs=3))
+        psum_h = stack.enter_context(tc.psum_pool(name="psum_h", bufs=HIDDEN // P))
+        psum_o = stack.enter_context(tc.psum_pool(name="psum_o", bufs=2))
 
         ident = keep.tile([P, P], BF16)
-        number_rows = keep.tile([P, CLAIMS], BF16)
+        number_x = keep.tile([P, CLAIMS], BF16)
         point_rows = keep.tile([P, 2 * CLAIMS], BF16)
         number_vecs = keep.tile([P, K_PASS], BF16)
         head_vecs = keep.tile([P, K_PASS], BF16)
         tail_vecs = keep.tile([P, K_PASS], BF16)
         b1_rows = keep.tile([P, P], BF16)
-        SEL_X, SEL_Y, SEL_NUMBER, SEL_TAIL = 0, 1, 2, 3
+        SEL_X, SEL_Y, SEL_TAIL = 0, 1, 2
         sel = keep.tile([P, SEL_TAIL + N_CHUNKS, P], BF16)
 
         w1_words = keep.tile([P, 2, HIDDEN], U32, align_bytes=64)
@@ -84,70 +84,76 @@ def tile_claimencoder_kernel(
         warm = keep.tile([P, 1], F32)
         nc.vector.memset(warm[:], 0.0)
         nc.scalar.activation(out=warm[:], in_=warm[:], func=ACT.Sin)
-        nc.vector.memset(number_rows[:], 0.0)
-        nc.vector.memset(number_vecs[:], 0.0)
-        nc.vector.memset(b1_rows[:], 0.0)
-        nc.vector.memset(sel[:], 0.0)
-        for r in range(3):
-            nc.vector.memset(sel[32 * r : 32 * r + 1, SEL_NUMBER, 32 * (r + 1) : 32 * (r + 2)], 1.0)
-        nc.vector.memset(point_rows[:], 0.0)
-        nc.vector.memset(head_vecs[:], 0.0)
-        nc.vector.memset(tail_vecs[:], 0.0)
-        half = 2 * QUARTER // PACK
-        nc.vector.memset(sel[0:1, SEL_X, 0:half], 1.0)
-        nc.vector.memset(sel[0:1, SEL_Y, half : 2 * half], 1.0)
-        nc.vector.memset(sel[32:33, SEL_X, 2 * half : 3 * half], 1.0)
-        nc.vector.memset(sel[32:33, SEL_Y, 3 * half : P], 1.0)
-        for i in range(N_CHUNKS):
-            quadrant = slice(TAIL_PARTITIONS * i, TAIL_PARTITIONS * (i + 1))
-            nc.vector.memset(sel[32:33, SEL_TAIL + i, quadrant], 1.0)
 
-        def load_row(queue, rows, row, first, vector):
+        def load_row(rows, row, first, vector):
             width = vector.shape[0]
-            queue.dma_start(out=rows[row : row + 1, first : first + width], in_=vector.unsqueeze(0))
+            nc.sync.dma_start(out=rows[row : row + 1, first : first + width], in_=vector.unsqueeze(0))
 
-        for r, numbers in enumerate((time_s, wait_src, wait_dst)):
-            load_row(nc.sync, number_rows, 32 * r, 0, numbers)
-        for r, (w, b) in enumerate(((t_w, t_b), (ws_w, ws_b), (wd_w, wd_b))):
-            first = TAIL + NUMBER_WIDTH * r
-            load_row(nc.sync, number_vecs, ROW_W, first, w)
-            load_row(nc.sync, number_vecs, ROW_B, first, b)
-
-        nc.sync.dma_start(out=b1_rows[0 : HIDDEN // P, :], in_=b1.rearrange("(mt m) -> mt m", m=P))
-        load_row(nc.sync, point_rows, 32, 0, dst_xy.rearrange("c two -> (c two)"))
-        load_row(nc.sync, point_rows, 0, 0, src_xy.rearrange("c two -> (c two)"))
-
-        def load_point_vector(queue, row, vector, first):
+        def load_point_vector(row, vector, first):
             head = max(0, min(QUARTER, K_PASS - first))
             if head > 0:
-                load_row(queue, head_vecs, row, first, vector[0:head])
+                load_row(head_vecs, row, first, vector[0:head])
             if head < QUARTER:
                 rest = QUARTER - head
                 at = first + head - K_PASS
                 copies = tail_vecs[row : row + 1, 0 : N_CHUNKS * TAIL].rearrange("o (i k) -> o i k", k=TAIL)
-                queue.dma_start(
+                nc.sync.dma_start(
                     out=copies[:, :, at : at + rest],
                     in_=vector[head:QUARTER].unsqueeze(0).unsqueeze(0).to_broadcast([1, N_CHUNKS, rest]),
                 )
+
+        def set_quarter_turn(first):
+            head = max(0, min(QUARTER, K_PASS - first))
+            if head > 0:
+                nc.vector.memset(head_vecs[ROW_PHASE : ROW_PHASE + 1, first : first + head], 0.25)
+            if head < QUARTER:
+                for i in range(N_CHUNKS):
+                    at = TAIL * i + first + head - K_PASS
+                    nc.vector.memset(tail_vecs[ROW_PHASE : ROW_PHASE + 1, at : at + QUARTER - head], 0.25)
 
         point_parts = (
             (src_wsx, src_bsx), (src_wcx, src_bcx), (src_wsy, src_bsy), (src_wcy, src_bcy),
             (dst_wsx, dst_bsx), (dst_wcx, dst_bcx), (dst_wsy, dst_bsy), (dst_wcy, dst_bcy),
         )
-        for q in reversed(range(len(point_parts))):
-            w, b = point_parts[q]
-            first = QUARTER * q
-            load_point_vector(nc.sync, ROW_W, w, first)
-            load_point_vector(nc.sync, ROW_B, b, first)
-            if q % 2 == 1:
-                head = max(0, min(QUARTER, K_PASS - first))
-                if head > 0:
-                    nc.vector.memset(head_vecs[ROW_PHASE : ROW_PHASE + 1, first : first + head], 0.25)
-                for i in range(N_CHUNKS):
-                    if head < QUARTER:
-                        at = TAIL * i + first + head - K_PASS
-                        nc.vector.memset(tail_vecs[ROW_PHASE : ROW_PHASE + 1, at : at + QUARTER - head], 0.25)
+        tail_parts = [q for q in range(len(point_parts)) if QUARTER * (q + 1) > K_PASS]
+        head_parts = [q for q in range(len(point_parts)) if q not in tail_parts]
 
+        def load_point_parts(parts):
+            for q in parts:
+                w, b = point_parts[q]
+                load_point_vector(ROW_W, w, QUARTER * q)
+                load_point_vector(ROW_B, b, QUARTER * q)
+                if q % 2 == 1:
+                    set_quarter_turn(QUARTER * q)
+
+        nc.vector.memset(point_rows[:], 0.0)
+        load_row(point_rows, 32, 0, dst_xy.rearrange("c two -> (c two)"))
+        load_row(point_rows, 0, 0, src_xy.rearrange("c two -> (c two)"))
+        nc.vector.memset(tail_vecs[:], 0.0)
+        nc.vector.memset(head_vecs[:], 0.0)
+        load_point_parts(tail_parts)
+        nc.vector.memset(sel[:], 0.0)
+        for i in range(N_CHUNKS):
+            quadrant = slice(TAIL_PARTITIONS * i, TAIL_PARTITIONS * (i + 1))
+            nc.vector.memset(sel[32:33, SEL_TAIL + i, quadrant], 1.0)
+
+        load_point_parts(head_parts)
+        half = 2 * QUARTER // PACK
+        nc.vector.memset(sel[0:1, SEL_X, 0:half], 1.0)
+        nc.vector.memset(sel[0:1, SEL_Y, half : 2 * half], 1.0)
+        nc.vector.memset(sel[32:33, SEL_X, 2 * half : 3 * half], 1.0)
+        nc.vector.memset(sel[32:33, SEL_Y, 3 * half : P], 1.0)
+
+        nc.vector.memset(number_x[0:TAIL_PARTITIONS, :], 0.0)
+        nc.vector.memset(number_vecs[:], 0.0)
+        for r, numbers in enumerate((time_s, wait_src, wait_dst)):
+            nc.sync.dma_start(out=number_x[32 * (r + 1) : 32 * (r + 2), :], in_=numbers.partition_broadcast(32))
+        for r, (w, b) in enumerate(((t_w, t_b), (ws_w, ws_b), (wd_w, wd_b))):
+            load_row(number_vecs, ROW_W, TAIL + NUMBER_WIDTH * r, w)
+            load_row(number_vecs, ROW_B, TAIL + NUMBER_WIDTH * r, b)
+
+        nc.vector.memset(b1_rows[:], 0.0)
+        nc.sync.dma_start(out=b1_rows[0 : HIDDEN // P, :], in_=b1.rearrange("(mt m) -> mt m", m=P))
         nc.sync.dma_start(
             out=w1_words[:].bitcast(I32),
             in_=W1_words.rearrange("g p n t -> p g (n t)").bitcast(I32),
@@ -177,13 +183,14 @@ def tile_claimencoder_kernel(
                 in_=W2_scales[0, 4 * quad : 4 * quad + 4, :].bitcast(I32),
             )
 
+        b1_cols = keep.tile([P, HIDDEN // P], F32)
         vecs_of = {"number": number_vecs, "head": head_vecs, "tail": tail_vecs}
         params_of = {}
 
         def prepare(kind):
             if kind in params_of:
                 return
-            turned = psum_t.tile([P, PACK, P], BF16, tag="turned")
+            turned = psum_o.tile([P, PACK, P], BF16, tag="o")
             for t in range(PACK):
                 nc.tensor.transpose(turned[:, t, :], vecs_of[kind][:, t : K_PASS : PACK], ident[:])
             params = keep.tile([P, PACK, N_ROWS], F32, name="params_" + kind)
@@ -210,8 +217,6 @@ def tile_claimencoder_kernel(
             kind, i = unit
             claims = slice(CHUNK * i, CHUNK * (i + 1))
             x = psum_x.tile([P, CHUNK], F32)
-            if kind == "number":
-                nc.tensor.matmul(x[:], lhsT=sel[:, SEL_NUMBER, :], rhs=number_rows[:, claims], start=True, stop=True)
             if kind == "head":
                 nc.tensor.matmul(x[:], lhsT=sel[:, SEL_X, :], rhs=xy[:, claims, 0], start=True, stop=False)
                 nc.tensor.matmul(x[:], lhsT=sel[:, SEL_Y, :], rhs=xy[:, claims, 1], start=False, stop=True)
@@ -224,17 +229,19 @@ def tile_claimencoder_kernel(
             x_of[unit] = x
 
         def make_lines(unit):
-            x = x_of[unit]
-            params = params_of[unit[0]]
-            lines = work.tile([P, PACK, CHUNK], F32)
+            kind, i = unit
+            params = params_of[kind]
+            lines = work.tile([P, PACK, CHUNK], F32, tag="lines_number" if kind == "number" else "lines")
             for t in range(PACK):
-                nc.scalar.activation(
-                    out=lines[:, t, :],
-                    in_=x[:],
-                    func=ACT.Identity,
-                    scale=params[:, t, ROW_W : ROW_W + 1],
-                    bias=params[:, t, ROW_B : ROW_B + 1],
-                )
+                w = params[:, t, ROW_W : ROW_W + 1]
+                b = params[:, t, ROW_B : ROW_B + 1]
+                if kind == "number":
+                    nc.gpsimd.tensor_scalar(
+                        out=lines[:, t, :], in0=number_x[:, CHUNK * i : CHUNK * (i + 1)],
+                        scalar1=w, scalar2=b, op0=ALU.mult, op1=ALU.add,
+                    )
+                else:
+                    nc.scalar.activation(out=lines[:, t, :], in_=x_of[unit][:], func=ACT.Identity, scale=w, bias=b)
             lines_of[unit] = lines
 
         def leaky_grouped(lines, grouped):
@@ -243,19 +250,24 @@ def tile_claimencoder_kernel(
                 out=grouped[:], in0=by_claim, scalar=SLOPE, in1=by_claim, op0=ALU.mult, op1=ALU.max
             )
 
-        def finish(unit):
+        def on_vector(unit):
             lines = lines_of[unit]
-            grouped = work.tile([P, CHUNK, PACK], BF16, align_bytes=64)
             if unit[0] == "number":
+                grouped = work.tile([P, CHUNK, PACK], BF16, align_bytes=64, tag="grouped_number")
                 leaky_grouped(lines, grouped)
+                grouped_of[unit] = grouped
             else:
-                whole = work.tile([P, PACK, CHUNK], I32)
+                whole = pair.tile([P, PACK, CHUNK], I32)
                 nc.vector.tensor_copy(out=whole[:], in_=lines[:])
                 nc.vector.tensor_tensor(out=lines[:], in0=lines[:], in1=whole[:], op=ALU.subtract)
+
+        def take_sine(unit):
+            if unit[0] != "number":
+                grouped = work.tile([P, CHUNK, PACK], BF16, align_bytes=64)
                 nc.scalar.activation(
-                    out=grouped[:], in_=lines[:].rearrange("p t c -> p c t"), func=ACT.Sin, scale=TURN
+                    out=grouped[:], in_=lines_of[unit][:].rearrange("p t c -> p c t"), func=ACT.Sin, scale=TURN
                 )
-            grouped_of[unit] = grouped
+                grouped_of[unit] = grouped
 
         def quantise(grouped, name):
             codes = keep.tile([P, CHUNK], U32, align_bytes=64, name="codes_" + name)
@@ -265,46 +277,49 @@ def tile_claimencoder_kernel(
             )
             return codes, scales
 
+        sums_of = {}
+
         def layer1(i):
             passes = (
                 (w1_words[:, 0, :], w1_scales[:, 0, :], ("head", i)),
                 (w1_words[:, 1, :], w1_scales[:, 1, :], ("number", i)),
                 (w1_tail_words[:, i, :], w1_tail_scales[:, i, :], ("tail", 0)),
             )
+            sums_of[i] = []
             for mt in range(HIDDEN // P):
-                units = slice(P * mt, P * (mt + 1))
+                units_mt = slice(P * mt, P * (mt + 1))
                 acc = psum_h.tile([P, CHUNK], F32)
                 for n, (words, scales, unit) in enumerate(passes):
                     nc.tensor.matmul_mx(
                         out=acc[:],
-                        lhsT=words[:, units].bitcast(FP8X4),
-                        lhsT_scale=scales[:, units],
+                        lhsT=words[:, units_mt].bitcast(FP8X4),
+                        lhsT_scale=scales[:, units_mt],
                         rhs=codes_of[unit][:].bitcast(FP8X4),
                         rhs_scale=scales_of[unit][:],
                         start=(n == 0),
                         stop=(n == len(passes) - 1),
                     )
+                sums_of[i].append(acc)
+
+        def regroup_hidden(i):
+            regrouped = work.tile([P, PACK, CHUNK], F32)
+            for mt in range(HIDDEN // P):
                 biased = stream.tile([P, CHUNK], F32)
                 nc.scalar.activation(
-                    out=biased[:], in_=acc[:], func=ACT.Identity, bias=b1_cols[:, mt : mt + 1], scale=1.0
+                    out=biased[:], in_=sums_of[i][mt][:], func=ACT.Identity, bias=b1_cols[:, mt : mt + 1], scale=1.0
                 )
-                first = CHUNK * i + P * mt
-                nc.sync.dma_start(out=out[first : first + P, :], in_=biased[:])
-            parked = work.tile([P, PACK, CHUNK], F32)
-            nc.sync.dma_start(
-                out=parked[:], in_=out[CHUNK * i : CHUNK * (i + 1), :].rearrange("(p t) c -> p t c", t=PACK)
-            )
-            lines_of[("hidden", i)] = parked
+                nc.sync.dma_start(out=regrouped[32 * mt : 32 * (mt + 1), :, :], in_=biased[:])
+            lines_of[("hidden", i)] = regrouped
 
         def finish_hidden(i):
-            h = work.tile([P, CHUNK, PACK], BF16, align_bytes=64)
+            h = pair.tile([P, CHUNK, PACK], BF16, align_bytes=64)
             leaky_grouped(lines_of[("hidden", i)], h)
             grouped_of[("hidden", i)] = h
 
         def layer2(i, codes, scales):
             for j in range(CHUNK // P):
                 claims = slice(P * j, P * (j + 1))
-                acc = psum_o.tile([P, OUT_WIDTH], F32)
+                acc = psum_o.tile([P, OUT_WIDTH], F32, tag="o")
                 nc.tensor.matmul_mx(
                     out=acc[:],
                     lhsT=codes[:, claims].bitcast(FP8X4),
@@ -328,32 +343,41 @@ def tile_claimencoder_kernel(
             codes, scales = quantise(grouped_of[("hidden", i)], "hidden%d" % i)
             layer2(i, codes, scales)
 
-        units = []
-        for i in range(N_CHUNKS):
-            units.append(("number", i))
-            if i == 0:
-                units.append(("tail", 0))
-            units.append(("head", i))
-        prepare(units[0][0])
-        b1_turned = psum_t.tile([P, P], BF16, tag="turned")
-        nc.tensor.transpose(b1_turned[:], b1_rows[:], ident[:])
-        b1_cols = keep.tile([P, HIDDEN // P], F32)
-        nc.vector.tensor_copy(out=b1_cols[:], in_=b1_turned[:, 0 : HIDDEN // P])
-        spread_claims(units[0])
-        for u in range(len(units) + 2):
-            if u + 1 < len(units):
-                spread_claims(units[u + 1])
-            if u < len(units):
-                make_lines(units[u])
-            if 0 <= u - 1 < len(units):
-                finish(units[u - 1])
-            if u >= 2:
-                unit = units[u - 2]
+        sines = [("tail", 0)] + [("head", i) for i in range(N_CHUNKS)]
+
+        def in_range(n, items):
+            return 0 <= n < len(items)
+
+        chunks = list(range(N_CHUNKS))
+        prepare("tail")
+        spread_claims(sines[0])
+        for r in range(len(sines) + 4):
+            if in_range(r + 1, sines):
+                spread_claims(sines[r + 1])
+            if in_range(r, sines):
+                make_lines(sines[r])
+            if r == 0:
+                prepare("head")
+            if in_range(r - 4, chunks):
+                regroup_hidden(r - 4)
+            if in_range(r - 1, sines):
+                on_vector(sines[r - 1])
+                take_sine(sines[r - 1])
+            if r == 1:
+                prepare("number")
+                b1_turned = psum_o.tile([P, P], BF16, tag="o")
+                nc.tensor.transpose(b1_turned[:], b1_rows[:], ident[:])
+                nc.vector.tensor_copy(out=b1_cols[:], in_=b1_turned[:, 0 : HIDDEN // P])
+            if in_range(r - 1, chunks):
+                make_lines(("number", r - 1))
+            if in_range(r - 2, sines):
+                unit = sines[r - 2]
                 codes_of[unit], scales_of[unit] = quantise(grouped_of[unit], "%s%d" % unit)
-                if unit[0] == "head":
-                    layer1(unit[1])
-                    if unit[1] > 0:
-                        second_half(unit[1] - 1)
-            if u + 1 < len(units):
-                prepare(units[u + 1][0])
-        second_half(N_CHUNKS - 1)
+            if in_range(r - 3, chunks):
+                unit = ("number", r - 3)
+                codes_of[unit], scales_of[unit] = quantise(grouped_of[unit], "%s%d" % unit)
+                layer1(r - 3)
+            if in_range(r - 2, chunks):
+                on_vector(("number", r - 2))
+            if in_range(r - 5, chunks):
+                second_half(r - 5)

@@ -53,6 +53,7 @@ def tile_claimencoder_kernel(
         work = stack.enter_context(tc.tile_pool(name="work", bufs=3))
         pair = stack.enter_context(tc.tile_pool(name="pair", bufs=2))
         stream = stack.enter_context(tc.tile_pool(name="stream", bufs=4))
+        late = stack.enter_context(tc.tile_pool(name="late", bufs=2 * CHUNK // P))
         psum_x = stack.enter_context(tc.psum_pool(name="psum_x", bufs=2))
         psum_h = stack.enter_context(tc.psum_pool(name="psum_h", bufs=HIDDEN // P))
         psum_o = stack.enter_context(tc.psum_pool(name="psum_o", bufs=2))
@@ -316,7 +317,10 @@ def tile_claimencoder_kernel(
             leaky_grouped(lines_of[("hidden", i)], h)
             grouped_of[("hidden", i)] = h
 
-        def layer2(i, codes, scales):
+        def layer2(i):
+            finish_hidden(i)
+            codes, scales = quantise(grouped_of[("hidden", i)], "hidden%d" % i)
+            sums_of[("out", i)] = []
             for j in range(CHUNK // P):
                 claims = slice(P * j, P * (j + 1))
                 acc = psum_o.tile([P, OUT_WIDTH], F32, tag="o")
@@ -329,19 +333,19 @@ def tile_claimencoder_kernel(
                     start=True,
                     stop=True,
                 )
-                z = stream.tile([P, OUT_WIDTH], F32)
+                z = late.tile([P, OUT_WIDTH], F32)
                 nc.vector.tensor_tensor(out=z[:], in0=acc[:], in1=b2_all[:], op=ALU.add)
+                sums_of[("out", i)].append(z)
+
+        def finish_out(i):
+            for j in range(CHUNK // P):
+                z = sums_of[("out", i)][j]
+                lift = stream.tile([P, OUT_WIDTH], F32)
+                nc.scalar.activation(out=lift[:], in_=z[:], func=ACT.Relu, scale=SLOPE - 1.0)
                 result = stream.tile([P, OUT_WIDTH], F32)
-                nc.vector.scalar_tensor_tensor(
-                    out=result[:], in0=z[:], scalar=SLOPE, in1=z[:], op0=ALU.mult, op1=ALU.max
-                )
+                nc.gpsimd.tensor_tensor(out=result[:], in0=z[:], in1=lift[:], op=ALU.add)
                 first = CHUNK * i + P * j
                 nc.sync.dma_start(out=out[first : first + P, :], in_=result[:])
-
-        def second_half(i):
-            finish_hidden(i)
-            codes, scales = quantise(grouped_of[("hidden", i)], "hidden%d" % i)
-            layer2(i, codes, scales)
 
         sines = [("tail", 0)] + [("head", i) for i in range(N_CHUNKS)]
 
@@ -351,7 +355,7 @@ def tile_claimencoder_kernel(
         chunks = list(range(N_CHUNKS))
         prepare("tail")
         spread_claims(sines[0])
-        for r in range(len(sines) + 4):
+        for r in range(len(sines) + 5):
             if in_range(r + 1, sines):
                 spread_claims(sines[r + 1])
             if in_range(r, sines):
@@ -379,5 +383,7 @@ def tile_claimencoder_kernel(
                 layer1(r - 3)
             if in_range(r - 2, chunks):
                 on_vector(("number", r - 2))
+            if in_range(r - 6, chunks):
+                finish_out(r - 6)
             if in_range(r - 5, chunks):
-                second_half(r - 5)
+                layer2(r - 5)

@@ -237,9 +237,9 @@ def tile_claimencoder_kernel(
                 w = params[:, t, ROW_W : ROW_W + 1]
                 b = params[:, t, ROW_B : ROW_B + 1]
                 if kind == "number":
-                    nc.gpsimd.tensor_scalar(
-                        out=lines[:, t, :], in0=number_x[:, CHUNK * i : CHUNK * (i + 1)],
-                        scalar1=w, scalar2=b, op0=ALU.mult, op1=ALU.add,
+                    nc.scalar.activation(
+                        out=lines[:, t, :], in_=number_x[:, CHUNK * i : CHUNK * (i + 1)],
+                        func=ACT.Identity, scale=w, bias=b,
                     )
                 else:
                     nc.scalar.activation(out=lines[:, t, :], in_=x_of[unit][:], func=ACT.Identity, scale=w, bias=b)
@@ -340,10 +340,10 @@ def tile_claimencoder_kernel(
         def finish_out(i):
             for j in range(CHUNK // P):
                 z = sums_of[("out", i)][j]
-                lift = stream.tile([P, OUT_WIDTH], F32)
-                nc.scalar.activation(out=lift[:], in_=z[:], func=ACT.Relu, scale=SLOPE - 1.0)
                 result = stream.tile([P, OUT_WIDTH], F32)
-                nc.gpsimd.tensor_tensor(out=result[:], in0=z[:], in1=lift[:], op=ALU.add)
+                nc.vector.scalar_tensor_tensor(
+                    out=result[:], in0=z[:], scalar=SLOPE, in1=z[:], op0=ALU.mult, op1=ALU.max
+                )
                 first = CHUNK * i + P * j
                 nc.sync.dma_start(out=out[first : first + P, :], in_=result[:])
 

@@ -34,6 +34,12 @@ ROW_W = 1
 ROW_B = 2
 N_ROWS = 3
 
+SRC_X = (0, 32)
+SRC_Y = (32, 32)
+DST_X = (64, 16)
+DST_Y = (80, 16)
+ONES = (96, 32)
+
 FLOPS = 2 * CLAIMS * (2 * K_PASS * HIDDEN + HIDDEN * OUT_WIDTH)
 
 
@@ -53,20 +59,20 @@ def tile_claimencoder_kernel(
         work = stack.enter_context(tc.tile_pool(name="work", bufs=3))
         pair = stack.enter_context(tc.tile_pool(name="pair", bufs=2))
         stream = stack.enter_context(tc.tile_pool(name="stream", bufs=4))
-        late = stack.enter_context(tc.tile_pool(name="late", bufs=2 * CHUNK // P))
-        psum_x = stack.enter_context(tc.psum_pool(name="psum_x", bufs=2))
-        psum_h = stack.enter_context(tc.psum_pool(name="psum_h", bufs=HIDDEN // P))
-        psum_o = stack.enter_context(tc.psum_pool(name="psum_o", bufs=2))
+        psum = stack.enter_context(tc.psum_pool(name="psum", bufs=8))
 
         ident = keep.tile([P, P], BF16)
         number_x = keep.tile([P, CLAIMS], BF16)
-        point_rows = keep.tile([P, 2 * CLAIMS], BF16)
-        number_vecs = keep.tile([P, K_PASS], BF16)
-        head_vecs = keep.tile([P, K_PASS], BF16)
+        number_wb = keep.tile([P, 2, 16], BF16)
+        number_params = keep.tile([P, 2, PACK], F32)
+        claim_rows = keep.tile([P, 2 * CLAIMS], BF16)
+        angle_vecs = keep.tile([P, K_PASS], BF16)
+        tail_x = keep.tile([P, 2 * CHUNK], BF16)
         tail_vecs = keep.tile([P, K_PASS], BF16)
         b1_rows = keep.tile([P, P], BF16)
-        SEL_X, SEL_Y, SEL_TAIL = 0, 1, 2
-        sel = keep.tile([P, SEL_TAIL + N_CHUNKS, P], BF16)
+        partition_index = keep.tile([P, 1], I32)
+        steps = keep.tile([P, 8], F32)
+        phase = keep.tile([P, 1], F32)
 
         w1_words = keep.tile([P, 2, HIDDEN], U32, align_bytes=64)
         w1_scales = keep.tile([P, 2, HIDDEN], U8, align_bytes=64)
@@ -76,85 +82,83 @@ def tile_claimencoder_kernel(
         w2_scales = keep.tile([P, OUT_WIDTH], U8, align_bytes=64)
         b2_all = keep.tile([P, OUT_WIDTH], BF16)
 
-        make_identity(nc, ident[:])
-        nc.gpsimd.dma_start(out=b2_all[:], in_=b2.partition_broadcast(P))
-        nc.gpsimd.memset(w1_scales[:].bitcast(F32), 0.0)
-        nc.gpsimd.memset(w1_tail_scales[:].bitcast(F32), 0.0)
-        nc.gpsimd.memset(w1_tail_words[:].bitcast(F32), 0.0)
-        nc.gpsimd.memset(w2_scales[:].bitcast(F32), 0.0)
         warm = keep.tile([P, 1], F32)
         nc.vector.memset(warm[:], 0.0)
+
+        for r, numbers in enumerate((time_s, wait_src, wait_dst)):
+            nc.sync.dma_start(out=number_x[32 * (r + 1) : 32 * (r + 2), :], in_=numbers.partition_broadcast(32))
+        nc.gpsimd.iota(partition_index[:], pattern=[[0, 1]], base=0, channel_multiplier=1)
+        for r, (w, b) in enumerate(((t_w, t_b), (ws_w, ws_b), (wd_w, wd_b))):
+            rows = slice(32 * (r + 1), 32 * (r + 2))
+            nc.scalar.dma_start(out=number_wb[rows, 0, 0:PACK], in_=w.rearrange("(p t) -> p t", t=PACK))
+            queue = nc.scalar if r < 2 else nc.gpsimd
+            queue.dma_start(out=number_wb[rows, 1, 0:PACK], in_=b.rearrange("(p t) -> p t", t=PACK))
         nc.scalar.activation(out=warm[:], in_=warm[:], func=ACT.Sin)
+        make_identity(nc, ident[:])
+        nc.vector.memset(tail_vecs[:], 0.0)
+        nc.vector.memset(number_wb[0:TAIL_PARTITIONS, :, :], 0.0)
+        nc.vector.memset(number_x[0:TAIL_PARTITIONS, :], 0.0)
+        nc.vector.memset(angle_vecs[:], 0.0)
 
-        def load_row(rows, row, first, vector):
-            width = vector.shape[0]
-            nc.sync.dma_start(out=rows[row : row + 1, first : first + width], in_=vector.unsqueeze(0))
-
-        def load_point_vector(row, vector, first):
+        src_flat = src_xy.rearrange("c two -> (c two)")
+        dst_flat = dst_xy.rearrange("c two -> (c two)")
+        point_parts = (
+            (src_wsx, src_bsx, SRC_X), (src_wcx, src_bcx, SRC_X), (src_wsy, src_bsy, SRC_Y), (src_wcy, src_bcy, SRC_Y),
+            (dst_wsx, dst_bsx, DST_X), (dst_wcx, dst_bcx, DST_X), (dst_wsy, dst_bsy, DST_Y), (dst_wcy, dst_bcy, DST_Y),
+        )
+        for i, (first, count) in enumerate(((0, 32), (32, 32), (64, 64))):
+            nc.sync.dma_start(
+                out=tail_x[first : first + count, :],
+                in_=dst_flat[2 * CHUNK * i : 2 * CHUNK * (i + 1)].partition_broadcast(count),
+            )
+        tail_copies = tail_vecs[:].rearrange("p (i k) -> p i k", k=TAIL)
+        for q, (w, b, rows) in enumerate(point_parts):
+            first = QUARTER * q
             head = max(0, min(QUARTER, K_PASS - first))
-            if head > 0:
-                load_row(head_vecs, row, first, vector[0:head])
             if head < QUARTER:
                 rest = QUARTER - head
                 at = first + head - K_PASS
-                copies = tail_vecs[row : row + 1, 0 : N_CHUNKS * TAIL].rearrange("o (i k) -> o i k", k=TAIL)
-                nc.sync.dma_start(
-                    out=copies[:, :, at : at + rest],
-                    in_=vector[head:QUARTER].unsqueeze(0).unsqueeze(0).to_broadcast([1, N_CHUNKS, rest]),
-                )
+                for row, vector in ((ROW_W, w), (ROW_B, b)):
+                    nc.sync.dma_start(
+                        out=tail_copies[row : row + 1, :, at : at + rest],
+                        in_=vector[head:QUARTER].unsqueeze(0).unsqueeze(0).to_broadcast([1, P // TAIL_PARTITIONS, rest]),
+                    )
+                if q % 2 == 1:
+                    nc.vector.memset(tail_copies[ROW_PHASE : ROW_PHASE + 1, :, at : at + rest], 0.25)
 
-        def set_quarter_turn(first):
+        for (first, count), flat, shift in ((SRC_X, src_flat, 0), (SRC_Y, src_flat, 1), (DST_X, dst_flat, 0), (DST_Y, dst_flat, 1)):
+            nc.sync.dma_start(
+                out=claim_rows[first : first + count, 0 : 2 * CLAIMS - shift],
+                in_=flat[shift : 2 * CLAIMS].partition_broadcast(count),
+            )
+        coordinate = claim_rows[:].rearrange("p (c two) -> p c two", two=2)
+        for i in range(N_CHUNKS):
+            nc.gpsimd.memset(claim_rows[ONES[0] : P, 2 * CHUNK * i : 2 * CHUNK * (i + 1)], 1.0)
+        nc.gpsimd.memset(w1_tail_words[:].bitcast(F32), 0.0)
+
+        for q, (w, b, (row, count)) in enumerate(point_parts):
+            first = QUARTER * q
             head = max(0, min(QUARTER, K_PASS - first))
             if head > 0:
-                nc.vector.memset(head_vecs[ROW_PHASE : ROW_PHASE + 1, first : first + head], 0.25)
-            if head < QUARTER:
-                for i in range(N_CHUNKS):
-                    at = TAIL * i + first + head - K_PASS
-                    nc.vector.memset(tail_vecs[ROW_PHASE : ROW_PHASE + 1, at : at + QUARTER - head], 0.25)
+                nc.sync.dma_start(out=angle_vecs[row : row + 1, first : first + head], in_=w[0:head].unsqueeze(0))
+                nc.sync.dma_start(out=angle_vecs[ONES[0] : ONES[0] + 1, first : first + head], in_=b[0:head].unsqueeze(0))
 
-        point_parts = (
-            (src_wsx, src_bsx), (src_wcx, src_bcx), (src_wsy, src_bsy), (src_wcy, src_bcy),
-            (dst_wsx, dst_bsx), (dst_wcx, dst_bcx), (dst_wsy, dst_bsy), (dst_wcy, dst_bcy),
+        part = QUARTER // PACK
+        nc.vector.tensor_scalar(
+            out=steps[:, 0:1], in0=partition_index[:], scalar1=float(part), scalar2=None, op0=ALU.is_ge
         )
-        tail_parts = [q for q in range(len(point_parts)) if QUARTER * (q + 1) > K_PASS]
-        head_parts = [q for q in range(len(point_parts)) if q not in tail_parts]
+        n_steps = K_PASS // QUARTER
+        for n in range(1, n_steps):
+            nc.vector.scalar_tensor_tensor(
+                out=steps[:, n : n + 1], in0=partition_index[:], scalar=float(part * (n + 1)), in1=steps[:, n - 1 : n],
+                op0=ALU.is_ge, op1=ALU.subtract,
+            )
+        nc.vector.tensor_scalar_mul(out=phase[:], in0=steps[:, n_steps - 1 : n_steps], scalar1=-0.25)
 
-        def load_point_parts(parts):
-            for q in parts:
-                w, b = point_parts[q]
-                load_point_vector(ROW_W, w, QUARTER * q)
-                load_point_vector(ROW_B, b, QUARTER * q)
-                if q % 2 == 1:
-                    set_quarter_turn(QUARTER * q)
-
-        nc.vector.memset(point_rows[:], 0.0)
-        load_row(point_rows, 32, 0, dst_xy.rearrange("c two -> (c two)"))
-        load_row(point_rows, 0, 0, src_xy.rearrange("c two -> (c two)"))
-        nc.vector.memset(tail_vecs[:], 0.0)
-        nc.vector.memset(head_vecs[:], 0.0)
-        load_point_parts(tail_parts)
-        nc.vector.memset(sel[:], 0.0)
-        for i in range(N_CHUNKS):
-            quadrant = slice(TAIL_PARTITIONS * i, TAIL_PARTITIONS * (i + 1))
-            nc.vector.memset(sel[32:33, SEL_TAIL + i, quadrant], 1.0)
-
-        load_point_parts(head_parts)
-        half = 2 * QUARTER // PACK
-        nc.vector.memset(sel[0:1, SEL_X, 0:half], 1.0)
-        nc.vector.memset(sel[0:1, SEL_Y, half : 2 * half], 1.0)
-        nc.vector.memset(sel[32:33, SEL_X, 2 * half : 3 * half], 1.0)
-        nc.vector.memset(sel[32:33, SEL_Y, 3 * half : P], 1.0)
-
-        nc.vector.memset(number_x[0:TAIL_PARTITIONS, :], 0.0)
-        nc.vector.memset(number_vecs[:], 0.0)
-        for r, numbers in enumerate((time_s, wait_src, wait_dst)):
-            nc.sync.dma_start(out=number_x[32 * (r + 1) : 32 * (r + 2), :], in_=numbers.partition_broadcast(32))
-        for r, (w, b) in enumerate(((t_w, t_b), (ws_w, ws_b), (wd_w, wd_b))):
-            load_row(number_vecs, ROW_W, TAIL + NUMBER_WIDTH * r, w)
-            load_row(number_vecs, ROW_B, TAIL + NUMBER_WIDTH * r, b)
-
+        nc.vector.memset(w1_scales[:].bitcast(I32), 0)
+        nc.vector.memset(w1_tail_scales[:].bitcast(I32), 0)
+        nc.vector.memset(w2_scales[:].bitcast(I32), 0)
         nc.vector.memset(b1_rows[:], 0.0)
-        nc.sync.dma_start(out=b1_rows[0 : HIDDEN // P, :], in_=b1.rearrange("(mt m) -> mt m", m=P))
         nc.sync.dma_start(
             out=w1_words[:].bitcast(I32),
             in_=W1_words.rearrange("g p n t -> p g (n t)").bitcast(I32),
@@ -174,6 +178,7 @@ def tile_claimencoder_kernel(
                 out=w1_tail_scales[base : base + 4, i, :].bitcast(I32),
                 in_=W1_scales[1, 0:4, :].bitcast(I32),
             )
+        nc.sync.dma_start(out=b1_rows[0 : HIDDEN // P, :], in_=b1.rearrange("(mt m) -> mt m", m=P))
         nc.sync.dma_start(
             out=w2_words[:].bitcast(I32),
             in_=W2_words[0].rearrange("p n t -> p (n t)").bitcast(I32),
@@ -183,67 +188,75 @@ def tile_claimencoder_kernel(
                 out=w2_scales[32 * quad : 32 * quad + 4, :].bitcast(I32),
                 in_=W2_scales[0, 4 * quad : 4 * quad + 4, :].bitcast(I32),
             )
+        nc.gpsimd.dma_start(out=b2_all[:], in_=b2.partition_broadcast(P))
 
         b1_cols = keep.tile([P, HIDDEN // P], F32)
-        vecs_of = {"number": number_vecs, "head": head_vecs, "tail": tail_vecs}
-        params_of = {}
-
-        def prepare(kind):
-            if kind in params_of:
-                return
-            turned = psum_o.tile([P, PACK, P], BF16, tag="o")
-            for t in range(PACK):
-                nc.tensor.transpose(turned[:, t, :], vecs_of[kind][:, t : K_PASS : PACK], ident[:])
-            params = keep.tile([P, PACK, N_ROWS], F32, name="params_" + kind)
-            nc.vector.tensor_copy(out=params[:], in_=turned[:, :, 0:N_ROWS])
-            if kind != "number":
-                nc.vector.tensor_scalar_mul(
-                    out=params[:, :, ROW_W : ROW_B + 1], in0=params[:, :, ROW_W : ROW_B + 1], scalar1=1.0 / TURN
-                )
-                nc.vector.tensor_add(
-                    out=params[:, :, ROW_B : ROW_B + 1],
-                    in0=params[:, :, ROW_B : ROW_B + 1],
-                    in1=params[:, :, ROW_PHASE : ROW_PHASE + 1],
-                )
-            params_of[kind] = params
-
-        xy = point_rows[:].rearrange("p (c two) -> p c two", two=2)
-        x_of = {}
+        tail_params = keep.tile([P, PACK, N_ROWS], F32)
+        angles_of = {}
+        whole_of = {}
         lines_of = {}
         grouped_of = {}
         codes_of = {}
         scales_of = {}
 
-        def spread_claims(unit):
-            kind, i = unit
-            claims = slice(CHUNK * i, CHUNK * (i + 1))
-            x = psum_x.tile([P, CHUNK], F32)
-            if kind == "head":
-                nc.tensor.matmul(x[:], lhsT=sel[:, SEL_X, :], rhs=xy[:, claims, 0], start=True, stop=False)
-                nc.tensor.matmul(x[:], lhsT=sel[:, SEL_Y, :], rhs=xy[:, claims, 1], start=False, stop=True)
-            if kind == "tail":
-                for j in range(N_CHUNKS):
-                    nc.tensor.matmul(
-                        x[:], lhsT=sel[:, SEL_TAIL + j, :], rhs=xy[:, CHUNK * j : CHUNK * (j + 1), 1],
-                        start=(j == 0), stop=(j == N_CHUNKS - 1),
-                    )
-            x_of[unit] = x
+        def prepare_number():
+            nc.vector.tensor_copy(out=number_params[:], in_=number_wb[:, :, 0:PACK])
 
-        def make_lines(unit):
-            kind, i = unit
-            params = params_of[kind]
-            lines = work.tile([P, PACK, CHUNK], F32, tag="lines_number" if kind == "number" else "lines")
+        def prepare_tail():
+            turned = psum.tile([P, PACK, P], BF16, tag="bank")
             for t in range(PACK):
-                w = params[:, t, ROW_W : ROW_W + 1]
-                b = params[:, t, ROW_B : ROW_B + 1]
-                if kind == "number":
-                    nc.scalar.activation(
-                        out=lines[:, t, :], in_=number_x[:, CHUNK * i : CHUNK * (i + 1)],
-                        func=ACT.Identity, scale=w, bias=b,
-                    )
-                else:
-                    nc.scalar.activation(out=lines[:, t, :], in_=x_of[unit][:], func=ACT.Identity, scale=w, bias=b)
-            lines_of[unit] = lines
+                nc.tensor.transpose(turned[:, t, :], tail_vecs[:, t : K_PASS : PACK], ident[:])
+            nc.vector.tensor_copy(out=tail_params[:], in_=turned[:, :, 0:N_ROWS])
+            nc.vector.tensor_scalar_mul(
+                out=tail_params[:, :, ROW_W : ROW_B + 1], in0=tail_params[:, :, ROW_W : ROW_B + 1], scalar1=1.0 / TURN
+            )
+            nc.vector.tensor_add(
+                out=tail_params[:, :, ROW_B : ROW_B + 1],
+                in0=tail_params[:, :, ROW_B : ROW_B + 1],
+                in1=tail_params[:, :, ROW_PHASE : ROW_PHASE + 1],
+            )
+
+        def prepare_b1():
+            b1_turned = psum.tile([P, P], BF16, tag="bank")
+            nc.tensor.transpose(b1_turned[:], b1_rows[:], ident[:])
+            nc.vector.tensor_copy(out=b1_cols[:], in_=b1_turned[:, 0 : HIDDEN // P])
+
+        def number_lines(i):
+            lines = work.tile([P, PACK, CHUNK], F32, tag="lines_number")
+            for t in range(PACK):
+                nc.scalar.activation(
+                    out=lines[:, t, :], in_=number_x[:, CHUNK * i : CHUNK * (i + 1)], func=ACT.Identity,
+                    scale=number_params[:, 0, t : t + 1], bias=number_params[:, 1, t : t + 1],
+                )
+            lines_of[("number", i)] = lines
+
+        def tail_lines():
+            lines = work.tile([P, PACK, CHUNK], F32, tag="lines")
+            y = tail_x[:].rearrange("p (c two) -> p c two", two=2)[:, :, 1]
+            for t in range(PACK):
+                nc.scalar.activation(
+                    out=lines[:, t, :], in_=y, func=ACT.Identity,
+                    scale=tail_params[:, t, ROW_W : ROW_W + 1], bias=tail_params[:, t, ROW_B : ROW_B + 1],
+                )
+            lines_of[("tail", 0)] = lines
+
+        def head_angles(i):
+            angles_of[i] = []
+            for t in range(PACK):
+                angle = psum.tile([P, CHUNK], F32, tag="bank")
+                nc.tensor.matmul(
+                    angle[:], lhsT=angle_vecs[:, t : K_PASS : PACK], rhs=coordinate[:, CHUNK * i : CHUNK * (i + 1), 0],
+                    start=True, stop=True,
+                )
+                angles_of[i].append(angle)
+
+        def head_lines(i):
+            lines = work.tile([P, PACK, CHUNK], F32, tag="lines")
+            for t in range(PACK):
+                nc.scalar.activation(
+                    out=lines[:, t, :], in_=angles_of[i][t][:], func=ACT.Identity, scale=1.0 / TURN, bias=phase[:]
+                )
+            lines_of[("head", i)] = lines
 
         def leaky_grouped(lines, grouped):
             by_claim = lines[:].rearrange("p t c -> p c t")
@@ -251,32 +264,35 @@ def tile_claimencoder_kernel(
                 out=grouped[:], in0=by_claim, scalar=SLOPE, in1=by_claim, op0=ALU.mult, op1=ALU.max
             )
 
-        def on_vector(unit):
+        def number_leaky(i):
+            grouped = work.tile([P, CHUNK, PACK], BF16, align_bytes=64, tag="grouped_number")
+            leaky_grouped(lines_of[("number", i)], grouped)
+            grouped_of[("number", i)] = grouped
+
+        def whole_turns(unit):
+            whole = pair.tile([P, PACK, CHUNK], I32)
+            nc.vector.tensor_copy(out=whole[:], in_=lines_of[unit][:])
+            whole_of[unit] = whole
+
+        def drop_turns(unit):
             lines = lines_of[unit]
-            if unit[0] == "number":
-                grouped = work.tile([P, CHUNK, PACK], BF16, align_bytes=64, tag="grouped_number")
-                leaky_grouped(lines, grouped)
-                grouped_of[unit] = grouped
-            else:
-                whole = pair.tile([P, PACK, CHUNK], I32)
-                nc.vector.tensor_copy(out=whole[:], in_=lines[:])
-                nc.vector.tensor_tensor(out=lines[:], in0=lines[:], in1=whole[:], op=ALU.subtract)
+            nc.vector.tensor_tensor(out=lines[:], in0=lines[:], in1=whole_of[unit][:], op=ALU.subtract)
 
         def take_sine(unit):
-            if unit[0] != "number":
-                grouped = work.tile([P, CHUNK, PACK], BF16, align_bytes=64)
-                nc.scalar.activation(
-                    out=grouped[:], in_=lines_of[unit][:].rearrange("p t c -> p c t"), func=ACT.Sin, scale=TURN
-                )
-                grouped_of[unit] = grouped
-
-        def quantise(grouped, name):
-            codes = keep.tile([P, CHUNK], U32, align_bytes=64, name="codes_" + name)
-            scales = keep.tile([P, CHUNK], U8, align_bytes=64, name="scales_" + name)
-            nc.vector.quantize_mx(
-                out=codes[:].bitcast(FP8X4), scales=scales[:], in_=grouped[:].rearrange("p c t -> p (c t)")
+            grouped = work.tile([P, CHUNK, PACK], BF16, align_bytes=64)
+            nc.scalar.activation(
+                out=grouped[:], in_=lines_of[unit][:].rearrange("p t c -> p c t"), func=ACT.Sin, scale=TURN
             )
-            return codes, scales
+            grouped_of[unit] = grouped
+
+        def quantise(unit):
+            codes = keep.tile([P, CHUNK], U32, align_bytes=64, name="codes_%s%d" % unit)
+            scales = keep.tile([P, CHUNK], U8, align_bytes=64, name="scales_%s%d" % unit)
+            nc.vector.quantize_mx(
+                out=codes[:].bitcast(FP8X4), scales=scales[:], in_=grouped_of[unit][:].rearrange("p c t -> p (c t)")
+            )
+            codes_of[unit] = codes
+            scales_of[unit] = scales
 
         sums_of = {}
 
@@ -289,7 +305,7 @@ def tile_claimencoder_kernel(
             sums_of[i] = []
             for mt in range(HIDDEN // P):
                 units_mt = slice(P * mt, P * (mt + 1))
-                acc = psum_h.tile([P, CHUNK], F32)
+                acc = psum.tile([P, CHUNK], F32, tag="bank")
                 for n, (words, scales, unit) in enumerate(passes):
                     nc.tensor.matmul_mx(
                         out=acc[:],
@@ -312,18 +328,17 @@ def tile_claimencoder_kernel(
                 nc.sync.dma_start(out=regrouped[32 * mt : 32 * (mt + 1), :, :], in_=biased[:])
             lines_of[("hidden", i)] = regrouped
 
-        def finish_hidden(i):
+        def hidden_leaky(i):
             h = pair.tile([P, CHUNK, PACK], BF16, align_bytes=64)
             leaky_grouped(lines_of[("hidden", i)], h)
             grouped_of[("hidden", i)] = h
 
         def layer2(i):
-            finish_hidden(i)
-            codes, scales = quantise(grouped_of[("hidden", i)], "hidden%d" % i)
-            sums_of[("out", i)] = []
+            codes, scales = codes_of[("hidden", i)], scales_of[("hidden", i)]
+            sums_of[("layer2", i)] = []
             for j in range(CHUNK // P):
                 claims = slice(P * j, P * (j + 1))
-                acc = psum_o.tile([P, OUT_WIDTH], F32, tag="o")
+                acc = psum.tile([P, OUT_WIDTH], F32, tag="bank")
                 nc.tensor.matmul_mx(
                     out=acc[:],
                     lhsT=codes[:, claims].bitcast(FP8X4),
@@ -333,57 +348,83 @@ def tile_claimencoder_kernel(
                     start=True,
                     stop=True,
                 )
-                z = late.tile([P, OUT_WIDTH], F32)
-                nc.vector.tensor_tensor(out=z[:], in0=acc[:], in1=b2_all[:], op=ALU.add)
-                sums_of[("out", i)].append(z)
+                sums_of[("layer2", i)].append(acc)
+
+        def add_b2(i):
+            z = pair.tile([P, CHUNK // P, OUT_WIDTH], F32)
+            for j in range(CHUNK // P):
+                nc.vector.tensor_tensor(out=z[:, j, :], in0=sums_of[("layer2", i)][j][:], in1=b2_all[:], op=ALU.add)
+            sums_of[("out", i)] = z
 
         def finish_out(i):
-            for j in range(CHUNK // P):
-                z = sums_of[("out", i)][j]
-                result = stream.tile([P, OUT_WIDTH], F32)
+            z = sums_of[("out", i)]
+            result = pair.tile([P, CHUNK // P, OUT_WIDTH], F32)
+            pieces = CHUNK // P if i == N_CHUNKS - 1 else 1
+            tiles = CHUNK // P // pieces
+            for n in range(pieces):
+                js = slice(tiles * n, tiles * (n + 1))
                 nc.vector.scalar_tensor_tensor(
-                    out=result[:], in0=z[:], scalar=SLOPE, in1=z[:], op0=ALU.mult, op1=ALU.max
+                    out=result[:, js, :], in0=z[:, js, :], scalar=SLOPE, in1=z[:, js, :], op0=ALU.mult, op1=ALU.max
                 )
-                first = CHUNK * i + P * j
-                nc.sync.dma_start(out=out[first : first + P, :], in_=result[:])
+                first = CHUNK * i + P * tiles * n
+                nc.sync.dma_start(
+                    out=out[first : first + P * tiles, :].rearrange("(j p) n -> p j n", p=P), in_=result[:, js, :]
+                )
 
-        sines = [("tail", 0)] + [("head", i) for i in range(N_CHUNKS)]
-
-        def in_range(n, items):
-            return 0 <= n < len(items)
-
-        chunks = list(range(N_CHUNKS))
-        prepare("tail")
-        spread_claims(sines[0])
-        for r in range(len(sines) + 5):
-            if in_range(r + 1, sines):
-                spread_claims(sines[r + 1])
-            if in_range(r, sines):
-                make_lines(sines[r])
-            if r == 0:
-                prepare("head")
-            if in_range(r - 4, chunks):
-                regroup_hidden(r - 4)
-            if in_range(r - 1, sines):
-                on_vector(sines[r - 1])
-                take_sine(sines[r - 1])
-            if r == 1:
-                prepare("number")
-                b1_turned = psum_o.tile([P, P], BF16, tag="o")
-                nc.tensor.transpose(b1_turned[:], b1_rows[:], ident[:])
-                nc.vector.tensor_copy(out=b1_cols[:], in_=b1_turned[:, 0 : HIDDEN // P])
-            if in_range(r - 1, chunks):
-                make_lines(("number", r - 1))
-            if in_range(r - 2, sines):
-                unit = sines[r - 2]
-                codes_of[unit], scales_of[unit] = quantise(grouped_of[unit], "%s%d" % unit)
-            if in_range(r - 3, chunks):
-                unit = ("number", r - 3)
-                codes_of[unit], scales_of[unit] = quantise(grouped_of[unit], "%s%d" % unit)
-                layer1(r - 3)
-            if in_range(r - 2, chunks):
-                on_vector(("number", r - 2))
-            if in_range(r - 6, chunks):
-                finish_out(r - 6)
-            if in_range(r - 5, chunks):
-                layer2(r - 5)
+        TAIL_UNIT = ("tail", 0)
+        prepare_number()
+        number_lines(0)
+        prepare_tail()
+        tail_lines()
+        number_leaky(0)
+        number_lines(1)
+        head_angles(0)
+        whole_turns(TAIL_UNIT)
+        head_lines(0)
+        drop_turns(TAIL_UNIT)
+        number_leaky(1)
+        take_sine(TAIL_UNIT)
+        head_angles(1)
+        whole_turns(("head", 0))
+        quantise(("number", 0))
+        head_lines(1)
+        head_angles(2)
+        drop_turns(("head", 0))
+        quantise(TAIL_UNIT)
+        quantise(("number", 1))
+        take_sine(("head", 0))
+        whole_turns(("head", 1))
+        number_lines(2)
+        head_lines(2)
+        prepare_b1()
+        quantise(("head", 0))
+        layer1(0)
+        drop_turns(("head", 1))
+        number_leaky(2)
+        regroup_hidden(0)
+        take_sine(("head", 1))
+        whole_turns(("head", 2))
+        quantise(("number", 2))
+        drop_turns(("head", 2))
+        quantise(("head", 1))
+        layer1(1)
+        take_sine(("head", 2))
+        regroup_hidden(1)
+        hidden_leaky(0)
+        quantise(("head", 2))
+        quantise(("hidden", 0))
+        layer2(0)
+        layer1(2)
+        add_b2(0)
+        regroup_hidden(2)
+        finish_out(0)
+        hidden_leaky(1)
+        quantise(("hidden", 1))
+        layer2(1)
+        add_b2(1)
+        hidden_leaky(2)
+        finish_out(1)
+        quantise(("hidden", 2))
+        layer2(2)
+        add_b2(2)
+        finish_out(2)

@@ -76,8 +76,6 @@ def tile_claimencoder_kernel(
 
         w1_words = keep.tile([P, 2, HIDDEN], U32, align_bytes=64)
         w1_scales = keep.tile([P, 2, HIDDEN], U8, align_bytes=64)
-        w1_tail_words = keep.tile([P, N_CHUNKS, HIDDEN], U32, align_bytes=64)
-        w1_tail_scales = keep.tile([P, N_CHUNKS, HIDDEN], U8, align_bytes=64)
         w2_words = keep.tile([P, OUT_WIDTH], U32, align_bytes=64)
         w2_scales = keep.tile([P, OUT_WIDTH], U8, align_bytes=64)
         b2_all = keep.tile([P, OUT_WIDTH], BF16)
@@ -96,6 +94,7 @@ def tile_claimencoder_kernel(
         nc.scalar.activation(out=warm[:], in_=warm[:], func=ACT.Sin)
         make_identity(nc, ident[:])
         nc.vector.memset(tail_vecs[:], 0.0)
+        nc.vector.memset(b1_rows[:], 0.0)
         nc.vector.memset(number_wb[0:TAIL_PARTITIONS, :, :], 0.0)
         nc.vector.memset(number_x[0:TAIL_PARTITIONS, :], 0.0)
         nc.vector.memset(angle_vecs[:], 0.0)
@@ -126,6 +125,8 @@ def tile_claimencoder_kernel(
                 if q % 2 == 1:
                     nc.vector.memset(tail_copies[ROW_PHASE : ROW_PHASE + 1, :, at : at + rest], 0.25)
 
+        nc.sync.dma_start(out=b1_rows[0 : HIDDEN // P, :], in_=b1.rearrange("(mt m) -> mt m", m=P))
+
         for (first, count), flat, shift in ((SRC_X, src_flat, 0), (SRC_Y, src_flat, 1), (DST_X, dst_flat, 0), (DST_Y, dst_flat, 1)):
             nc.sync.dma_start(
                 out=claim_rows[first : first + count, 0 : 2 * CLAIMS - shift],
@@ -134,7 +135,6 @@ def tile_claimencoder_kernel(
         coordinate = claim_rows[:].rearrange("p (c two) -> p c two", two=2)
         for i in range(N_CHUNKS):
             nc.gpsimd.memset(claim_rows[ONES[0] : P, 2 * CHUNK * i : 2 * CHUNK * (i + 1)], 1.0)
-        nc.gpsimd.memset(w1_tail_words[:].bitcast(F32), 0.0)
 
         for q, (w, b, (row, count)) in enumerate(point_parts):
             first = QUARTER * q
@@ -156,9 +156,7 @@ def tile_claimencoder_kernel(
         nc.vector.tensor_scalar_mul(out=phase[:], in0=steps[:, n_steps - 1 : n_steps], scalar1=-0.25)
 
         nc.vector.memset(w1_scales[:].bitcast(I32), 0)
-        nc.vector.memset(w1_tail_scales[:].bitcast(I32), 0)
         nc.vector.memset(w2_scales[:].bitcast(I32), 0)
-        nc.vector.memset(b1_rows[:], 0.0)
         nc.sync.dma_start(
             out=w1_words[:].bitcast(I32),
             in_=W1_words.rearrange("g p n t -> p g (n t)").bitcast(I32),
@@ -168,17 +166,6 @@ def tile_claimencoder_kernel(
                 out=w1_scales[32 * quad : 32 * quad + 4, :, :].bitcast(I32),
                 in_=W1_scales[:, 4 * quad : 4 * quad + 4, :].rearrange("g r n -> r g n").bitcast(I32),
             )
-        for i in range(N_CHUNKS):
-            base = TAIL_PARTITIONS * i
-            nc.sync.dma_start(
-                out=w1_tail_words[base : base + TAIL_PARTITIONS, i, :].bitcast(I32),
-                in_=W1_words[1, 0:TAIL_PARTITIONS].rearrange("p n t -> p (n t)").bitcast(I32),
-            )
-            nc.sync.dma_start(
-                out=w1_tail_scales[base : base + 4, i, :].bitcast(I32),
-                in_=W1_scales[1, 0:4, :].bitcast(I32),
-            )
-        nc.sync.dma_start(out=b1_rows[0 : HIDDEN // P, :], in_=b1.rearrange("(mt m) -> mt m", m=P))
         nc.sync.dma_start(
             out=w2_words[:].bitcast(I32),
             in_=W2_words[0].rearrange("p n t -> p (n t)").bitcast(I32),
@@ -203,10 +190,12 @@ def tile_claimencoder_kernel(
             nc.vector.tensor_copy(out=number_params[:], in_=number_wb[:, :, 0:PACK])
 
         def prepare_tail():
-            turned = psum.tile([P, PACK, P], BF16, tag="bank")
+            turned = psum.tile([P, PACK + 1, P], BF16, tag="bank")
             for t in range(PACK):
                 nc.tensor.transpose(turned[:, t, :], tail_vecs[:, t : K_PASS : PACK], ident[:])
-            nc.vector.tensor_copy(out=tail_params[:], in_=turned[:, :, 0:N_ROWS])
+            nc.tensor.transpose(turned[:, PACK, :], b1_rows[:], ident[:])
+            nc.vector.tensor_copy(out=tail_params[:], in_=turned[:, 0:PACK, 0:N_ROWS])
+            nc.vector.tensor_copy(out=b1_cols[:], in_=turned[:, PACK, 0 : HIDDEN // P])
             nc.vector.tensor_scalar_mul(
                 out=tail_params[:, :, ROW_W : ROW_B + 1], in0=tail_params[:, :, ROW_W : ROW_B + 1], scalar1=1.0 / TURN
             )
@@ -216,18 +205,16 @@ def tile_claimencoder_kernel(
                 in1=tail_params[:, :, ROW_PHASE : ROW_PHASE + 1],
             )
 
-        def prepare_b1():
-            b1_turned = psum.tile([P, P], BF16, tag="bank")
-            nc.tensor.transpose(b1_turned[:], b1_rows[:], ident[:])
-            nc.vector.tensor_copy(out=b1_cols[:], in_=b1_turned[:, 0 : HIDDEN // P])
-
         def number_lines(i):
             lines = work.tile([P, PACK, CHUNK], F32, tag="lines_number")
             for t in range(PACK):
-                nc.scalar.activation(
-                    out=lines[:, t, :], in_=number_x[:, CHUNK * i : CHUNK * (i + 1)], func=ACT.Identity,
-                    scale=number_params[:, 0, t : t + 1], bias=number_params[:, 1, t : t + 1],
-                )
+                x = number_x[:, CHUNK * i : CHUNK * (i + 1)]
+                w = number_params[:, 0, t : t + 1]
+                b = number_params[:, 1, t : t + 1]
+                if i == 0:
+                    nc.vector.tensor_scalar(out=lines[:, t, :], in0=x, scalar1=w, scalar2=b, op0=ALU.mult, op1=ALU.add)
+                else:
+                    nc.scalar.activation(out=lines[:, t, :], in_=x, func=ACT.Identity, scale=w, bias=b)
             lines_of[("number", i)] = lines
 
         def tail_lines():
@@ -269,6 +256,12 @@ def tile_claimencoder_kernel(
             leaky_grouped(lines_of[("number", i)], grouped)
             grouped_of[("number", i)] = grouped
 
+        def move_tail(i):
+            nc.sync.dma_start(
+                out=grouped_of[("number", i)][0:TAIL_PARTITIONS, :, :],
+                in_=grouped_of[TAIL_UNIT][TAIL_PARTITIONS * i : TAIL_PARTITIONS * (i + 1), :, :],
+            )
+
         def whole_turns(unit):
             whole = pair.tile([P, PACK, CHUNK], I32)
             nc.vector.tensor_copy(out=whole[:], in_=lines_of[unit][:])
@@ -296,27 +289,21 @@ def tile_claimencoder_kernel(
 
         sums_of = {}
 
-        def layer1(i):
-            passes = (
-                (w1_words[:, 0, :], w1_scales[:, 0, :], ("head", i)),
-                (w1_words[:, 1, :], w1_scales[:, 1, :], ("number", i)),
-                (w1_tail_words[:, i, :], w1_tail_scales[:, i, :], ("tail", 0)),
-            )
-            sums_of[i] = []
+        def layer1(i, opening):
+            if opening:
+                sums_of[i] = [psum.tile([P, CHUNK], F32, tag="bank", name="acc%d_%d" % (i, mt)) for mt in range(HIDDEN // P)]
+            g, unit = (1, ("number", i)) if opening else (0, ("head", i))
             for mt in range(HIDDEN // P):
                 units_mt = slice(P * mt, P * (mt + 1))
-                acc = psum.tile([P, CHUNK], F32, tag="bank")
-                for n, (words, scales, unit) in enumerate(passes):
-                    nc.tensor.matmul_mx(
-                        out=acc[:],
-                        lhsT=words[:, units_mt].bitcast(FP8X4),
-                        lhsT_scale=scales[:, units_mt],
-                        rhs=codes_of[unit][:].bitcast(FP8X4),
-                        rhs_scale=scales_of[unit][:],
-                        start=(n == 0),
-                        stop=(n == len(passes) - 1),
-                    )
-                sums_of[i].append(acc)
+                nc.tensor.matmul_mx(
+                    out=sums_of[i][mt][:],
+                    lhsT=w1_words[:, g, units_mt].bitcast(FP8X4),
+                    lhsT_scale=w1_scales[:, g, units_mt],
+                    rhs=codes_of[unit][:].bitcast(FP8X4),
+                    rhs_scale=scales_of[unit][:],
+                    start=opening,
+                    stop=not opening,
+                )
 
         def regroup_hidden(i):
             regrouped = work.tile([P, PACK, CHUNK], F32)
@@ -374,57 +361,61 @@ def tile_claimencoder_kernel(
         TAIL_UNIT = ("tail", 0)
         prepare_number()
         number_lines(0)
+        number_lines(1)
+        number_leaky(0)
         prepare_tail()
         tail_lines()
-        number_leaky(0)
-        number_lines(1)
-        head_angles(0)
-        whole_turns(TAIL_UNIT)
-        head_lines(0)
-        drop_turns(TAIL_UNIT)
         number_leaky(1)
-        take_sine(TAIL_UNIT)
-        head_angles(1)
+        head_angles(0)
+        head_lines(0)
+        whole_turns(TAIL_UNIT)
+        number_lines(2)
+        drop_turns(TAIL_UNIT)
         whole_turns(("head", 0))
-        quantise(("number", 0))
+        take_sine(TAIL_UNIT)
+        move_tail(0)
+        move_tail(1)
+        head_angles(1)
+        drop_turns(("head", 0))
         head_lines(1)
         head_angles(2)
-        drop_turns(("head", 0))
-        quantise(TAIL_UNIT)
-        quantise(("number", 1))
-        take_sine(("head", 0))
-        whole_turns(("head", 1))
-        number_lines(2)
-        head_lines(2)
-        prepare_b1()
-        quantise(("head", 0))
-        layer1(0)
-        drop_turns(("head", 1))
         number_leaky(2)
+        move_tail(2)
+        take_sine(("head", 0))
+        quantise(("number", 0))
+        layer1(0, True)
+        whole_turns(("head", 1))
+        quantise(("number", 1))
+        head_lines(2)
+        quantise(("head", 0))
+        layer1(0, False)
+        drop_turns(("head", 1))
         regroup_hidden(0)
         take_sine(("head", 1))
+        layer1(1, True)
         whole_turns(("head", 2))
-        quantise(("number", 2))
         drop_turns(("head", 2))
         quantise(("head", 1))
-        layer1(1)
+        layer1(1, False)
         take_sine(("head", 2))
         regroup_hidden(1)
+        quantise(("number", 2))
         hidden_leaky(0)
+        layer1(2, True)
         quantise(("head", 2))
         quantise(("hidden", 0))
         layer2(0)
-        layer1(2)
+        layer1(2, False)
         add_b2(0)
         regroup_hidden(2)
-        finish_out(0)
         hidden_leaky(1)
+        finish_out(0)
         quantise(("hidden", 1))
         layer2(1)
-        add_b2(1)
         hidden_leaky(2)
-        finish_out(1)
+        add_b2(1)
         quantise(("hidden", 2))
         layer2(2)
+        finish_out(1)
         add_b2(2)
         finish_out(2)

@@ -58,7 +58,6 @@ def tile_claimencoder_kernel(
         stack.enter_context(tc.manual_schedule())
         work = stack.enter_context(tc.tile_pool(name="work", bufs=3))
         pair = stack.enter_context(tc.tile_pool(name="pair", bufs=2))
-        stream = stack.enter_context(tc.tile_pool(name="stream", bufs=4))
         psum = stack.enter_context(tc.psum_pool(name="psum", bufs=8))
 
         ident = keep.tile([P, P], BF16)
@@ -69,11 +68,13 @@ def tile_claimencoder_kernel(
         angle_vecs = keep.tile([P, K_PASS], BF16)
         tail_x = keep.tile([P, 2 * CHUNK], BF16)
         tail_vecs = keep.tile([P, K_PASS], BF16)
-        b1_rows = keep.tile([P, P], BF16)
+        b1_cols = keep.tile([P, PACK], BF16)
         partition_index = keep.tile([P, 1], I32)
         steps = keep.tile([P, 8], F32)
         phase = keep.tile([P, 1], F32)
 
+        w1_loaded_words = keep.tile([P, 2, HIDDEN], U32, align_bytes=64)
+        w1_loaded_scales = keep.tile([P, 2, HIDDEN], U8, align_bytes=64)
         w1_words = keep.tile([P, 2, HIDDEN], U32, align_bytes=64)
         w1_scales = keep.tile([P, 2, HIDDEN], U8, align_bytes=64)
         w2_words = keep.tile([P, OUT_WIDTH], U32, align_bytes=64)
@@ -94,7 +95,6 @@ def tile_claimencoder_kernel(
         nc.scalar.activation(out=warm[:], in_=warm[:], func=ACT.Sin)
         make_identity(nc, ident[:])
         nc.vector.memset(tail_vecs[:], 0.0)
-        nc.vector.memset(b1_rows[:], 0.0)
         nc.vector.memset(number_wb[0:TAIL_PARTITIONS, :, :], 0.0)
         nc.vector.memset(number_x[0:TAIL_PARTITIONS, :], 0.0)
         nc.vector.memset(angle_vecs[:], 0.0)
@@ -125,7 +125,6 @@ def tile_claimencoder_kernel(
                 if q % 2 == 1:
                     nc.vector.memset(tail_copies[ROW_PHASE : ROW_PHASE + 1, :, at : at + rest], 0.25)
 
-        nc.sync.dma_start(out=b1_rows[0 : HIDDEN // P, :], in_=b1.rearrange("(mt m) -> mt m", m=P))
 
         for (first, count), flat, shift in ((SRC_X, src_flat, 0), (SRC_Y, src_flat, 1), (DST_X, dst_flat, 0), (DST_Y, dst_flat, 1)):
             nc.sync.dma_start(
@@ -155,17 +154,18 @@ def tile_claimencoder_kernel(
             )
         nc.vector.tensor_scalar_mul(out=phase[:], in0=steps[:, n_steps - 1 : n_steps], scalar1=-0.25)
 
-        nc.vector.memset(w1_scales[:].bitcast(I32), 0)
+        nc.vector.memset(w1_loaded_scales[:].bitcast(I32), 0)
         nc.vector.memset(w2_scales[:].bitcast(I32), 0)
         nc.sync.dma_start(
-            out=w1_words[:].bitcast(I32),
+            out=w1_loaded_words[:].bitcast(I32),
             in_=W1_words.rearrange("g p n t -> p g (n t)").bitcast(I32),
         )
         for quad in range(4):
             nc.sync.dma_start(
-                out=w1_scales[32 * quad : 32 * quad + 4, :, :].bitcast(I32),
+                out=w1_loaded_scales[32 * quad : 32 * quad + 4, :, :].bitcast(I32),
                 in_=W1_scales[:, 4 * quad : 4 * quad + 4, :].rearrange("g r n -> r g n").bitcast(I32),
             )
+        nc.sync.dma_start(out=b1_cols[:], in_=b1.rearrange("(p t) -> p t", t=PACK))
         nc.sync.dma_start(
             out=w2_words[:].bitcast(I32),
             in_=W2_words[0].rearrange("p n t -> p (n t)").bitcast(I32),
@@ -177,7 +177,6 @@ def tile_claimencoder_kernel(
             )
         nc.gpsimd.dma_start(out=b2_all[:], in_=b2.partition_broadcast(P))
 
-        b1_cols = keep.tile([P, HIDDEN // P], F32)
         tail_params = keep.tile([P, PACK, N_ROWS], F32)
         angles_of = {}
         whole_of = {}
@@ -190,12 +189,10 @@ def tile_claimencoder_kernel(
             nc.vector.tensor_copy(out=number_params[:], in_=number_wb[:, :, 0:PACK])
 
         def prepare_tail():
-            turned = psum.tile([P, PACK + 1, P], BF16, tag="bank")
+            turned = psum.tile([P, PACK, P], BF16, tag="bank")
             for t in range(PACK):
                 nc.tensor.transpose(turned[:, t, :], tail_vecs[:, t : K_PASS : PACK], ident[:])
-            nc.tensor.transpose(turned[:, PACK, :], b1_rows[:], ident[:])
-            nc.vector.tensor_copy(out=tail_params[:], in_=turned[:, 0:PACK, 0:N_ROWS])
-            nc.vector.tensor_copy(out=b1_cols[:], in_=turned[:, PACK, 0 : HIDDEN // P])
+            nc.vector.tensor_copy(out=tail_params[:], in_=turned[:, :, 0:N_ROWS])
             nc.vector.tensor_scalar_mul(
                 out=tail_params[:, :, ROW_W : ROW_B + 1], in0=tail_params[:, :, ROW_W : ROW_B + 1], scalar1=1.0 / TURN
             )
@@ -289,6 +286,16 @@ def tile_claimencoder_kernel(
 
         sums_of = {}
 
+        def permute_w1():
+            nc.vector.tensor_copy(
+                out=w1_words[:].bitcast(I32).rearrange("p g (t m) -> p g t m", t=PACK),
+                in_=w1_loaded_words[:].bitcast(I32).rearrange("p g (m t) -> p g t m", t=PACK),
+            )
+            nc.vector.tensor_copy(
+                out=w1_scales[:].rearrange("p g (t m) -> p g t m", t=PACK),
+                in_=w1_loaded_scales[:].rearrange("p g (m t) -> p g t m", t=PACK),
+            )
+
         def layer1(i, opening):
             if opening:
                 sums_of[i] = [psum.tile([P, CHUNK], F32, tag="bank", name="acc%d_%d" % (i, mt)) for mt in range(HIDDEN // P)]
@@ -307,12 +314,10 @@ def tile_claimencoder_kernel(
 
         def regroup_hidden(i):
             regrouped = work.tile([P, PACK, CHUNK], F32)
-            for mt in range(HIDDEN // P):
-                biased = stream.tile([P, CHUNK], F32)
+            for t in range(PACK):
                 nc.scalar.activation(
-                    out=biased[:], in_=sums_of[i][mt][:], func=ACT.Identity, bias=b1_cols[:, mt : mt + 1], scale=1.0
+                    out=regrouped[:, t, :], in_=sums_of[i][t][:], func=ACT.Identity, bias=b1_cols[:, t : t + 1], scale=1.0
                 )
-                nc.sync.dma_start(out=regrouped[32 * mt : 32 * (mt + 1), :, :], in_=biased[:])
             lines_of[("hidden", i)] = regrouped
 
         def hidden_leaky(i):
@@ -366,52 +371,53 @@ def tile_claimencoder_kernel(
         prepare_tail()
         tail_lines()
         number_leaky(1)
+        number_lines(2)
+        whole_turns(TAIL_UNIT)
         head_angles(0)
         head_lines(0)
-        whole_turns(TAIL_UNIT)
-        number_lines(2)
         drop_turns(TAIL_UNIT)
-        whole_turns(("head", 0))
+        number_leaky(2)
+        head_angles(1)
         take_sine(TAIL_UNIT)
         move_tail(0)
         move_tail(1)
-        head_angles(1)
-        drop_turns(("head", 0))
+        move_tail(2)
+        whole_turns(("head", 0))
         head_lines(1)
         head_angles(2)
-        number_leaky(2)
-        move_tail(2)
+        drop_turns(("head", 0))
+        permute_w1()
         take_sine(("head", 0))
+        whole_turns(("head", 1))
         quantise(("number", 0))
         layer1(0, True)
-        whole_turns(("head", 1))
-        quantise(("number", 1))
+        drop_turns(("head", 1))
         head_lines(2)
+        quantise(("number", 1))
         quantise(("head", 0))
         layer1(0, False)
-        drop_turns(("head", 1))
-        regroup_hidden(0)
-        take_sine(("head", 1))
         layer1(1, True)
+        take_sine(("head", 1))
         whole_turns(("head", 2))
+        regroup_hidden(0)
+        quantise(("number", 2))
         drop_turns(("head", 2))
         quantise(("head", 1))
         layer1(1, False)
-        take_sine(("head", 2))
-        regroup_hidden(1)
-        quantise(("number", 2))
-        hidden_leaky(0)
         layer1(2, True)
+        take_sine(("head", 2))
+        hidden_leaky(0)
+        regroup_hidden(1)
         quantise(("head", 2))
+        layer1(2, False)
         quantise(("hidden", 0))
         layer2(0)
-        layer1(2, False)
-        add_b2(0)
         regroup_hidden(2)
         hidden_leaky(1)
-        finish_out(0)
+        add_b2(0)
         quantise(("hidden", 1))
         layer2(1)
+        finish_out(0)
         hidden_leaky(2)
         add_b2(1)
         quantise(("hidden", 2))

@@ -271,7 +271,9 @@ def tile_claimencoder_kernel(
         def take_sine(unit):
             grouped = work.tile([P, CHUNK, PACK], BF16, align_bytes=64)
             nc.scalar.activation(
-                out=grouped[:], in_=lines_of[unit][:].rearrange("p t c -> p c t"), func=ACT.Sin, scale=TURN
+                out=grouped[:].rearrange("p (c i) t -> p c t i", i=4),
+                in_=lines_of[unit][:].rearrange("p t (c i) -> p c t i", i=4),
+                func=ACT.Sin, scale=TURN,
             )
             grouped_of[unit] = grouped
 

@@ -34,11 +34,14 @@ ROW_W = 1
 ROW_B = 2
 N_ROWS = 3
 
-SRC_X = (0, 32)
-SRC_Y = (32, 32)
-DST_X = (64, 16)
-DST_Y = (80, 16)
-ONES = (96, 32)
+SRC_X = 0
+SRC_Y = 1
+DST_X = 2
+DST_Y = 3
+ONES = 32
+
+QUADRANTS = P // TAIL_PARTITIONS
+TAIL_CLAIMS = CLAIMS // QUADRANTS
 
 FLOPS = 2 * CLAIMS * (2 * K_PASS * HIDDEN + HIDDEN * OUT_WIDTH)
 
@@ -66,7 +69,8 @@ def tile_claimencoder_kernel(
         number_params = keep.tile([P, 2, PACK], F32)
         claim_rows = keep.tile([P, 2 * CLAIMS], BF16)
         angle_vecs = keep.tile([P, K_PASS], BF16)
-        tail_x = keep.tile([P, 2 * CHUNK], BF16)
+        tail_rows = keep.tile([P, 2 * TAIL_CLAIMS], BF16)
+        spread = keep.tile([P, P], BF16)
         tail_vecs = keep.tile([P, K_PASS], BF16)
         b1_cols = keep.tile([P, PACK], BF16)
         partition_index = keep.tile([P, 1], I32)
@@ -93,11 +97,17 @@ def tile_claimencoder_kernel(
             queue = nc.scalar if r < 2 else nc.gpsimd
             queue.dma_start(out=number_wb[rows, 1, 0:PACK], in_=b.rearrange("(p t) -> p t", t=PACK))
         nc.scalar.activation(out=warm[:], in_=warm[:], func=ACT.Sin)
+        nc.gpsimd.memset(number_x[0:TAIL_PARTITIONS, :].bitcast(F32), 0.0)
         make_identity(nc, ident[:])
+        nc.vector.memset(tail_rows[:], 0.0)
         nc.vector.memset(tail_vecs[:], 0.0)
         nc.vector.memset(number_wb[0:TAIL_PARTITIONS, :, :], 0.0)
-        nc.vector.memset(number_x[0:TAIL_PARTITIONS, :], 0.0)
         nc.vector.memset(angle_vecs[:], 0.0)
+        nc.vector.memset(spread[:], 0.0)
+        for j in range(QUADRANTS):
+            rows = slice(TAIL_PARTITIONS * j, TAIL_PARTITIONS * (j + 1))
+            nc.vector.memset(spread[TAIL_PARTITIONS * j : TAIL_PARTITIONS * j + 1, rows], 1.0)
+        nc.gpsimd.memset(claim_rows[:].bitcast(F32), 0.0)
 
         src_flat = src_xy.rearrange("c two -> (c two)")
         dst_flat = dst_xy.rearrange("c two -> (c two)")
@@ -105,11 +115,7 @@ def tile_claimencoder_kernel(
             (src_wsx, src_bsx, SRC_X), (src_wcx, src_bcx, SRC_X), (src_wsy, src_bsy, SRC_Y), (src_wcy, src_bcy, SRC_Y),
             (dst_wsx, dst_bsx, DST_X), (dst_wcx, dst_bcx, DST_X), (dst_wsy, dst_bsy, DST_Y), (dst_wcy, dst_bcy, DST_Y),
         )
-        for i, (first, count) in enumerate(((0, 32), (32, 32), (64, 64))):
-            nc.sync.dma_start(
-                out=tail_x[first : first + count, :],
-                in_=dst_flat[2 * CHUNK * i : 2 * CHUNK * (i + 1)].partition_broadcast(count),
-            )
+        nc.sync.dma_start(out=tail_rows[0:P:TAIL_PARTITIONS, :], in_=dst_flat.rearrange("(j e) -> j e", j=QUADRANTS))
         tail_copies = tail_vecs[:].rearrange("p (i k) -> p i k", k=TAIL)
         for q, (w, b, rows) in enumerate(point_parts):
             first = QUARTER * q
@@ -120,27 +126,25 @@ def tile_claimencoder_kernel(
                 for row, vector in ((ROW_W, w), (ROW_B, b)):
                     nc.sync.dma_start(
                         out=tail_copies[row : row + 1, :, at : at + rest],
-                        in_=vector[head:QUARTER].unsqueeze(0).unsqueeze(0).to_broadcast([1, P // TAIL_PARTITIONS, rest]),
+                        in_=vector[head:QUARTER].unsqueeze(0).unsqueeze(0).to_broadcast([1, QUADRANTS, rest]),
                     )
                 if q % 2 == 1:
                     nc.vector.memset(tail_copies[ROW_PHASE : ROW_PHASE + 1, :, at : at + rest], 0.25)
 
 
-        for (first, count), flat, shift in ((SRC_X, src_flat, 0), (SRC_Y, src_flat, 1), (DST_X, dst_flat, 0), (DST_Y, dst_flat, 1)):
-            nc.sync.dma_start(
-                out=claim_rows[first : first + count, 0 : 2 * CLAIMS - shift],
-                in_=flat[shift : 2 * CLAIMS].partition_broadcast(count),
-            )
-        coordinate = claim_rows[:].rearrange("p (c two) -> p c two", two=2)
-        for i in range(N_CHUNKS):
-            nc.gpsimd.memset(claim_rows[ONES[0] : P, 2 * CHUNK * i : 2 * CHUNK * (i + 1)], 1.0)
-
-        for q, (w, b, (row, count)) in enumerate(point_parts):
+        for q, (w, b, row) in enumerate(point_parts):
             first = QUARTER * q
             head = max(0, min(QUARTER, K_PASS - first))
             if head > 0:
                 nc.sync.dma_start(out=angle_vecs[row : row + 1, first : first + head], in_=w[0:head].unsqueeze(0))
-                nc.sync.dma_start(out=angle_vecs[ONES[0] : ONES[0] + 1, first : first + head], in_=b[0:head].unsqueeze(0))
+                nc.sync.dma_start(out=angle_vecs[ONES : ONES + 1, first : first + head], in_=b[0:head].unsqueeze(0))
+        for row, flat, shift in ((SRC_X, src_flat, 0), (SRC_Y, src_flat, 1), (DST_X, dst_flat, 0), (DST_Y, dst_flat, 1)):
+            nc.sync.dma_start(
+                out=claim_rows[row : row + 1, 0 : 2 * CLAIMS - shift], in_=flat[shift : 2 * CLAIMS].unsqueeze(0)
+            )
+        coordinate = claim_rows[:].rearrange("p (c two) -> p c two", two=2)
+        for i in range(N_CHUNKS):
+            nc.gpsimd.memset(claim_rows[ONES : ONES + 1, 2 * CHUNK * i : 2 * CHUNK * (i + 1)], 1.0)
 
         part = QUARTER // PACK
         nc.vector.tensor_scalar(
@@ -192,6 +196,12 @@ def tile_claimencoder_kernel(
             turned = psum.tile([P, PACK, P], BF16, tag="bank")
             for t in range(PACK):
                 nc.tensor.transpose(turned[:, t, :], tail_vecs[:, t : K_PASS : PACK], ident[:])
+            y_of_tail = psum.tile([P, TAIL_CLAIMS], F32, tag="bank")
+            nc.tensor.matmul(
+                y_of_tail[:], lhsT=spread[:], rhs=tail_rows[:].rearrange("p (c two) -> p c two", two=2)[:, :, 1],
+                start=True, stop=True,
+            )
+            angles_of["tail"] = y_of_tail
             nc.vector.tensor_copy(out=tail_params[:], in_=turned[:, :, 0:N_ROWS])
             nc.vector.tensor_scalar_mul(
                 out=tail_params[:, :, ROW_W : ROW_B + 1], in0=tail_params[:, :, ROW_W : ROW_B + 1], scalar1=1.0 / TURN
@@ -215,11 +225,10 @@ def tile_claimencoder_kernel(
             lines_of[("number", i)] = lines
 
         def tail_lines():
-            lines = work.tile([P, PACK, CHUNK], F32, tag="lines")
-            y = tail_x[:].rearrange("p (c two) -> p c two", two=2)[:, :, 1]
+            lines = work.tile([P, PACK, TAIL_CLAIMS], F32, tag="lines")
             for t in range(PACK):
                 nc.scalar.activation(
-                    out=lines[:, t, :], in_=y, func=ACT.Identity,
+                    out=lines[:, t, :], in_=angles_of["tail"][:], func=ACT.Identity,
                     scale=tail_params[:, t, ROW_W : ROW_W + 1], bias=tail_params[:, t, ROW_B : ROW_B + 1],
                 )
             lines_of[("tail", 0)] = lines
@@ -253,14 +262,23 @@ def tile_claimencoder_kernel(
             leaky_grouped(lines_of[("number", i)], grouped)
             grouped_of[("number", i)] = grouped
 
+        def width_of(unit):
+            return TAIL_CLAIMS if unit[0] == "tail" else CHUNK
+
         def move_tail(i):
-            nc.sync.dma_start(
-                out=grouped_of[("number", i)][0:TAIL_PARTITIONS, :, :],
-                in_=grouped_of[TAIL_UNIT][TAIL_PARTITIONS * i : TAIL_PARTITIONS * (i + 1), :, :],
-            )
+            for j in range(QUADRANTS):
+                first = max(CHUNK * i, TAIL_CLAIMS * j)
+                last = min(CHUNK * (i + 1), TAIL_CLAIMS * (j + 1))
+                if first < last:
+                    nc.sync.dma_start(
+                        out=grouped_of[("number", i)][0:TAIL_PARTITIONS, first - CHUNK * i : last - CHUNK * i, :],
+                        in_=grouped_of[TAIL_UNIT][
+                            TAIL_PARTITIONS * j : TAIL_PARTITIONS * (j + 1), first - TAIL_CLAIMS * j : last - TAIL_CLAIMS * j, :
+                        ],
+                    )
 
         def whole_turns(unit):
-            whole = pair.tile([P, PACK, CHUNK], I32)
+            whole = pair.tile([P, PACK, width_of(unit)], I32)
             nc.vector.tensor_copy(out=whole[:], in_=lines_of[unit][:])
             whole_of[unit] = whole
 
@@ -269,7 +287,7 @@ def tile_claimencoder_kernel(
             nc.vector.tensor_tensor(out=lines[:], in0=lines[:], in1=whole_of[unit][:], op=ALU.subtract)
 
         def take_sine(unit):
-            grouped = work.tile([P, CHUNK, PACK], BF16, align_bytes=64)
+            grouped = work.tile([P, width_of(unit), PACK], BF16, align_bytes=64)
             nc.scalar.activation(
                 out=grouped[:].rearrange("p (c i) t -> p c t i", i=4),
                 in_=lines_of[unit][:].rearrange("p t (c i) -> p c t i", i=4),

@@ -35,10 +35,10 @@ ROW_B = 2
 N_ROWS = 3
 
 SRC_X = 0
-SRC_Y = 1
-DST_X = 2
-DST_Y = 3
-ONES = 32
+SRC_Y = 32
+DST_X = 64
+DST_Y = 96
+MARK = 32
 
 QUADRANTS = P // TAIL_PARTITIONS
 TAIL_CLAIMS = CLAIMS // QUADRANTS
@@ -69,12 +69,12 @@ def tile_claimencoder_kernel(
         number_params = keep.tile([P, 2, PACK], F32)
         claim_rows = keep.tile([P, 2 * CLAIMS], BF16)
         angle_vecs = keep.tile([P, K_PASS], BF16)
+        shift_vecs = keep.tile([P, K_PASS], BF16)
+        head_bias = keep.tile([P, PACK], F32)
         tail_rows = keep.tile([P, 2 * TAIL_CLAIMS], BF16)
         spread = keep.tile([P, P], BF16)
         tail_vecs = keep.tile([P, K_PASS], BF16)
         b1_cols = keep.tile([P, PACK], BF16)
-        partition_index = keep.tile([P, 1], I32)
-        steps = keep.tile([P, 8], F32)
         phase = keep.tile([P, 1], F32)
 
         w1_loaded_words = keep.tile([P, 2, HIDDEN], U32, align_bytes=64)
@@ -88,26 +88,30 @@ def tile_claimencoder_kernel(
         warm = keep.tile([P, 1], F32)
         nc.vector.memset(warm[:], 0.0)
 
-        for r, numbers in enumerate((time_s, wait_src, wait_dst)):
-            nc.sync.dma_start(out=number_x[32 * (r + 1) : 32 * (r + 2), :], in_=numbers.partition_broadcast(32))
-        nc.gpsimd.iota(partition_index[:], pattern=[[0, 1]], base=0, channel_multiplier=1)
+        for first, count, numbers in ((0, 64, time_s), (64, 32, wait_src), (96, 32, wait_dst)):
+            nc.sync.dma_start(out=number_x[first : first + count, :], in_=numbers.partition_broadcast(count))
         for r, (w, b) in enumerate(((t_w, t_b), (ws_w, ws_b), (wd_w, wd_b))):
             rows = slice(32 * (r + 1), 32 * (r + 2))
             nc.scalar.dma_start(out=number_wb[rows, 0, 0:PACK], in_=w.rearrange("(p t) -> p t", t=PACK))
             queue = nc.scalar if r < 2 else nc.gpsimd
             queue.dma_start(out=number_wb[rows, 1, 0:PACK], in_=b.rearrange("(p t) -> p t", t=PACK))
         nc.scalar.activation(out=warm[:], in_=warm[:], func=ACT.Sin)
-        nc.gpsimd.memset(number_x[0:TAIL_PARTITIONS, :].bitcast(F32), 0.0)
+        nc.gpsimd.memset(w1_loaded_scales[:].bitcast(F32), 0.0)
+        nc.gpsimd.memset(w2_scales[:].bitcast(F32), 0.0)
         make_identity(nc, ident[:])
         nc.vector.memset(tail_rows[:], 0.0)
         nc.vector.memset(tail_vecs[:], 0.0)
         nc.vector.memset(number_wb[0:TAIL_PARTITIONS, :, :], 0.0)
         nc.vector.memset(angle_vecs[:], 0.0)
+        nc.vector.memset(shift_vecs[:], 0.0)
+        parts = shift_vecs[MARK : MARK + 1, 0 : 2 * QUARTER * (K_PASS // (2 * QUARTER))].rearrange(
+            "o (h q k) -> o h q k", q=2, k=QUARTER
+        )
+        nc.vector.memset(parts[:, :, 1, :], 0.25)
         nc.vector.memset(spread[:], 0.0)
         for j in range(QUADRANTS):
             rows = slice(TAIL_PARTITIONS * j, TAIL_PARTITIONS * (j + 1))
             nc.vector.memset(spread[TAIL_PARTITIONS * j : TAIL_PARTITIONS * j + 1, rows], 1.0)
-        nc.gpsimd.memset(claim_rows[:].bitcast(F32), 0.0)
 
         src_flat = src_xy.rearrange("c two -> (c two)")
         dst_flat = dst_xy.rearrange("c two -> (c two)")
@@ -137,29 +141,14 @@ def tile_claimencoder_kernel(
             head = max(0, min(QUARTER, K_PASS - first))
             if head > 0:
                 nc.sync.dma_start(out=angle_vecs[row : row + 1, first : first + head], in_=w[0:head].unsqueeze(0))
-                nc.sync.dma_start(out=angle_vecs[ONES : ONES + 1, first : first + head], in_=b[0:head].unsqueeze(0))
+                nc.sync.dma_start(out=shift_vecs[0:1, first : first + head], in_=b[0:head].unsqueeze(0))
         for row, flat, shift in ((SRC_X, src_flat, 0), (SRC_Y, src_flat, 1), (DST_X, dst_flat, 0), (DST_Y, dst_flat, 1)):
             nc.sync.dma_start(
-                out=claim_rows[row : row + 1, 0 : 2 * CLAIMS - shift], in_=flat[shift : 2 * CLAIMS].unsqueeze(0)
+                out=claim_rows[row : row + TAIL_PARTITIONS, 0 : 2 * CLAIMS - shift],
+                in_=flat[shift : 2 * CLAIMS].partition_broadcast(TAIL_PARTITIONS),
             )
         coordinate = claim_rows[:].rearrange("p (c two) -> p c two", two=2)
-        for i in range(N_CHUNKS):
-            nc.gpsimd.memset(claim_rows[ONES : ONES + 1, 2 * CHUNK * i : 2 * CHUNK * (i + 1)], 1.0)
 
-        part = QUARTER // PACK
-        nc.vector.tensor_scalar(
-            out=steps[:, 0:1], in0=partition_index[:], scalar1=float(part), scalar2=None, op0=ALU.is_ge
-        )
-        n_steps = K_PASS // QUARTER
-        for n in range(1, n_steps):
-            nc.vector.scalar_tensor_tensor(
-                out=steps[:, n : n + 1], in0=partition_index[:], scalar=float(part * (n + 1)), in1=steps[:, n - 1 : n],
-                op0=ALU.is_ge, op1=ALU.subtract,
-            )
-        nc.vector.tensor_scalar_mul(out=phase[:], in0=steps[:, n_steps - 1 : n_steps], scalar1=-0.25)
-
-        nc.vector.memset(w1_loaded_scales[:].bitcast(I32), 0)
-        nc.vector.memset(w2_scales[:].bitcast(I32), 0)
         nc.sync.dma_start(
             out=w1_loaded_words[:].bitcast(I32),
             in_=W1_words.rearrange("g p n t -> p g (n t)").bitcast(I32),
@@ -179,7 +168,7 @@ def tile_claimencoder_kernel(
                 out=w2_scales[32 * quad : 32 * quad + 4, :].bitcast(I32),
                 in_=W2_scales[0, 4 * quad : 4 * quad + 4, :].bitcast(I32),
             )
-        nc.gpsimd.dma_start(out=b2_all[:], in_=b2.partition_broadcast(P))
+        nc.sync.dma_start(out=b2_all[:], in_=b2.partition_broadcast(P))
 
         tail_params = keep.tile([P, PACK, N_ROWS], F32)
         angles_of = {}
@@ -233,6 +222,21 @@ def tile_claimencoder_kernel(
                 )
             lines_of[("tail", 0)] = lines
 
+        def prepare_head():
+            shifts = psum.tile([P, PACK + 1], F32, tag="bank")
+            for t in range(PACK):
+                nc.tensor.matmul(
+                    shifts[:, t : t + 1], lhsT=shift_vecs[:, t : K_PASS : PACK], rhs=ident[:, 0:1], start=True, stop=True
+                )
+            nc.tensor.matmul(
+                shifts[:, PACK : PACK + 1], lhsT=shift_vecs[:, 0:K_PASS:PACK], rhs=ident[:, MARK : MARK + 1],
+                start=True, stop=True,
+            )
+            nc.scalar.copy(out=phase[:], in_=shifts[:, PACK : PACK + 1])
+            nc.scalar.activation(
+                out=head_bias[:], in_=shifts[:, 0:PACK], func=ACT.Identity, scale=1.0 / TURN, bias=phase[:]
+            )
+
         def head_angles(i):
             angles_of[i] = []
             for t in range(PACK):
@@ -247,7 +251,8 @@ def tile_claimencoder_kernel(
             lines = work.tile([P, PACK, CHUNK], F32, tag="lines")
             for t in range(PACK):
                 nc.scalar.activation(
-                    out=lines[:, t, :], in_=angles_of[i][t][:], func=ACT.Identity, scale=1.0 / TURN, bias=phase[:]
+                    out=lines[:, t, :], in_=angles_of[i][t][:], func=ACT.Identity, scale=1.0 / TURN,
+                    bias=head_bias[:, t : t + 1],
                 )
             lines_of[("head", i)] = lines
 
@@ -393,6 +398,7 @@ def tile_claimencoder_kernel(
         number_leaky(1)
         number_lines(2)
         whole_turns(TAIL_UNIT)
+        prepare_head()
         head_angles(0)
         head_lines(0)
         drop_turns(TAIL_UNIT)

@@ -39,6 +39,7 @@ SRC_Y = 32
 DST_X = 64
 DST_Y = 96
 MARK = 32
+B2_ROW = 64
 
 QUADRANTS = P // TAIL_PARTITIONS
 TAIL_CLAIMS = CLAIMS // QUADRANTS
@@ -71,6 +72,9 @@ def tile_claimencoder_kernel(
         angle_vecs = keep.tile([P, K_PASS], BF16)
         shift_vecs = keep.tile([P, K_PASS], BF16)
         head_bias = keep.tile([P, PACK], F32)
+        ident_f32 = keep.tile([P, P], F32)
+        b2_cols = keep.tile([P, OUT_WIDTH // P], F32)
+        b2_low = keep.tile([P, OUT_WIDTH // P], F32)
         tail_rows = keep.tile([P, 2 * TAIL_CLAIMS], BF16)
         spread = keep.tile([P, P], BF16)
         tail_vecs = keep.tile([P, K_PASS], BF16)
@@ -142,6 +146,7 @@ def tile_claimencoder_kernel(
             if head > 0:
                 nc.sync.dma_start(out=angle_vecs[row : row + 1, first : first + head], in_=w[0:head].unsqueeze(0))
                 nc.sync.dma_start(out=shift_vecs[0:1, first : first + head], in_=b[0:head].unsqueeze(0))
+        nc.sync.dma_start(out=shift_vecs[B2_ROW : B2_ROW + 1, :], in_=b2.unsqueeze(0))
         for row, flat, shift in ((SRC_X, src_flat, 0), (SRC_Y, src_flat, 1), (DST_X, dst_flat, 0), (DST_Y, dst_flat, 1)):
             nc.sync.dma_start(
                 out=claim_rows[row : row + TAIL_PARTITIONS, 0 : 2 * CLAIMS - shift],
@@ -202,7 +207,7 @@ def tile_claimencoder_kernel(
             )
 
         def number_lines(i):
-            lines = work.tile([P, PACK, CHUNK], F32, tag="lines_number")
+            lines = pair.tile([P, PACK, CHUNK], F32, tag="lines_number")
             for t in range(PACK):
                 x = number_x[:, CHUNK * i : CHUNK * (i + 1)]
                 w = number_params[:, 0, t : t + 1]
@@ -223,7 +228,8 @@ def tile_claimencoder_kernel(
             lines_of[("tail", 0)] = lines
 
         def prepare_head():
-            shifts = psum.tile([P, PACK + 1], F32, tag="bank")
+            n_tiles = OUT_WIDTH // P
+            shifts = psum.tile([P, PACK + 1 + n_tiles], F32, tag="bank")
             for t in range(PACK):
                 nc.tensor.matmul(
                     shifts[:, t : t + 1], lhsT=shift_vecs[:, t : K_PASS : PACK], rhs=ident[:, 0:1], start=True, stop=True
@@ -232,7 +238,13 @@ def tile_claimencoder_kernel(
                 shifts[:, PACK : PACK + 1], lhsT=shift_vecs[:, 0:K_PASS:PACK], rhs=ident[:, MARK : MARK + 1],
                 start=True, stop=True,
             )
+            for nt in range(n_tiles):
+                nc.tensor.matmul(
+                    shifts[:, PACK + 1 + nt : PACK + 2 + nt], lhsT=shift_vecs[:, P * nt : P * (nt + 1)],
+                    rhs=ident[:, B2_ROW : B2_ROW + 1], start=True, stop=True,
+                )
             nc.scalar.copy(out=phase[:], in_=shifts[:, PACK : PACK + 1])
+            nc.scalar.copy(out=b2_cols[:], in_=shifts[:, PACK + 1 : PACK + 1 + n_tiles])
             nc.scalar.activation(
                 out=head_bias[:], in_=shifts[:, 0:PACK], func=ACT.Identity, scale=1.0 / TURN, bias=phase[:]
             )
@@ -338,7 +350,7 @@ def tile_claimencoder_kernel(
                 )
 
         def regroup_hidden(i):
-            regrouped = work.tile([P, PACK, CHUNK], F32)
+            regrouped = pair.tile([P, PACK, CHUNK], F32)
             for t in range(PACK):
                 nc.scalar.activation(
                     out=regrouped[:, t, :], in_=sums_of[i][t][:], func=ACT.Identity, bias=b1_cols[:, t : t + 1], scale=1.0
@@ -367,8 +379,64 @@ def tile_claimencoder_kernel(
                 )
                 sums_of[("layer2", i)].append(acc)
 
+        def prepare_turned():
+            nc.scalar.copy(out=ident_f32[:], in_=ident[:])
+            nc.scalar.mul(out=b2_low[:], in_=b2_cols[:], mul=SLOPE)
+
+        def layer2_turned(i):
+            codes, scales = codes_of[("hidden", i)], scales_of[("hidden", i)]
+            sums_of[("layer2", i)] = []
+            for nt in range(OUT_WIDTH // P):
+                channels = slice(P * nt, P * (nt + 1))
+                acc = psum.tile([P, CHUNK], F32, tag="bank")
+                nc.tensor.matmul_mx(
+                    out=acc[:],
+                    lhsT=w2_words[:, channels].bitcast(FP8X4),
+                    lhsT_scale=w2_scales[:, channels],
+                    rhs=codes[:].bitcast(FP8X4),
+                    rhs_scale=scales[:],
+                    start=True,
+                    stop=True,
+                )
+                sums_of[("layer2", i)].append(acc)
+
+        def lower_out(i):
+            low = pair.tile([P, OUT_WIDTH // P, CHUNK], F32, tag="z")
+            for nt in range(OUT_WIDTH // P):
+                nc.scalar.activation(
+                    out=low[:, nt, :], in_=sums_of[("layer2", i)][nt][:], func=ACT.Identity, scale=SLOPE,
+                    bias=b2_low[:, nt : nt + 1],
+                )
+            sums_of[("low", i)] = low
+
+        def max_out(i):
+            channels_first = pair.tile([P, OUT_WIDTH // P, CHUNK], F32)
+            for nt in range(OUT_WIDTH // P):
+                nc.vector.scalar_tensor_tensor(
+                    out=channels_first[:, nt, :], in0=sums_of[("layer2", i)][nt][:], scalar=b2_cols[:, nt : nt + 1],
+                    in1=sums_of[("low", i)][:, nt, :], op0=ALU.add, op1=ALU.max,
+                )
+            sums_of[("out", i)] = channels_first
+
+        def turn_out(i):
+            sums_of[("turned", i)] = []
+            for j in range(CHUNK // P):
+                bank = psum.tile([P, OUT_WIDTH], F32, tag="bank")
+                for nt in range(OUT_WIDTH // P):
+                    nc.tensor.transpose(
+                        bank[:, P * nt : P * (nt + 1)], sums_of[("out", i)][:, nt, P * j : P * (j + 1)], ident_f32[:]
+                    )
+                sums_of[("turned", i)].append(bank)
+
+        def store_turned(i):
+            claims_first = pair.tile([P, CHUNK // P, OUT_WIDTH], F32)
+            for j in range(CHUNK // P):
+                nc.scalar.copy(out=claims_first[:, j, :], in_=sums_of[("turned", i)][j][:])
+                first = CHUNK * i + P * j
+                nc.sync.dma_start(out=out[first : first + P, :], in_=claims_first[:, j, :])
+
         def add_b2(i):
-            z = pair.tile([P, CHUNK // P, OUT_WIDTH], F32)
+            z = pair.tile([P, CHUNK // P, OUT_WIDTH], F32, tag="z")
             for j in range(CHUNK // P):
                 nc.vector.tensor_tensor(out=z[:, j, :], in0=sums_of[("layer2", i)][j][:], in1=b2_all[:], op=ALU.add)
             sums_of[("out", i)] = z
@@ -437,17 +505,22 @@ def tile_claimencoder_kernel(
         quantise(("head", 2))
         layer1(2, False)
         quantise(("hidden", 0))
-        layer2(0)
+        layer2_turned(0)
         regroup_hidden(2)
+        prepare_turned()
+        lower_out(0)
         hidden_leaky(1)
-        add_b2(0)
         quantise(("hidden", 1))
-        layer2(1)
-        finish_out(0)
+        max_out(0)
+        layer2_turned(1)
+        turn_out(0)
         hidden_leaky(2)
-        add_b2(1)
+        lower_out(1)
+        store_turned(0)
         quantise(("hidden", 2))
+        max_out(1)
         layer2(2)
-        finish_out(1)
+        turn_out(1)
         add_b2(2)
+        store_turned(1)
         finish_out(2)

@@ -176,6 +176,7 @@ def tile_claimencoder_kernel(
         nc.sync.dma_start(out=b2_all[:], in_=b2.partition_broadcast(P))
 
         tail_params = keep.tile([P, PACK, N_ROWS], F32)
+        tail_phase = keep.tile([P, 1], F32)
         angles_of = {}
         whole_of = {}
         lines_of = {}
@@ -184,7 +185,7 @@ def tile_claimencoder_kernel(
         scales_of = {}
 
         def prepare_number():
-            nc.vector.tensor_copy(out=number_params[:], in_=number_wb[:, :, 0:PACK])
+            nc.scalar.copy(out=number_params[:], in_=number_wb[:, :, 0:PACK])
 
         def prepare_tail():
             turned = psum.tile([P, PACK, P], BF16, tag="bank")
@@ -196,26 +197,26 @@ def tile_claimencoder_kernel(
                 start=True, stop=True,
             )
             angles_of["tail"] = y_of_tail
-            nc.vector.tensor_copy(out=tail_params[:], in_=turned[:, :, 0:N_ROWS])
-            nc.vector.tensor_scalar_mul(
-                out=tail_params[:, :, ROW_W : ROW_B + 1], in0=tail_params[:, :, ROW_W : ROW_B + 1], scalar1=1.0 / TURN
-            )
-            nc.vector.tensor_add(
-                out=tail_params[:, :, ROW_B : ROW_B + 1],
-                in0=tail_params[:, :, ROW_B : ROW_B + 1],
-                in1=tail_params[:, :, ROW_PHASE : ROW_PHASE + 1],
+            nc.scalar.copy(out=tail_phase[:], in_=turned[:, 0, ROW_PHASE : ROW_PHASE + 1])
+            nc.scalar.mul(out=tail_params[:, :, ROW_W], in_=turned[:, :, ROW_W], mul=1.0 / TURN)
+            nc.scalar.activation(
+                out=tail_params[:, :, ROW_B], in_=turned[:, :, ROW_B], func=ACT.Identity, scale=1.0 / TURN, bias=tail_phase[:]
             )
 
         def number_lines(i):
             lines = pair.tile([P, PACK, CHUNK], F32, tag="lines_number")
             for t in range(PACK):
                 x = number_x[:, CHUNK * i : CHUNK * (i + 1)]
-                w = number_params[:, 0, t : t + 1]
-                b = number_params[:, 1, t : t + 1]
                 if i == 0:
-                    nc.vector.tensor_scalar(out=lines[:, t, :], in0=x, scalar1=w, scalar2=b, op0=ALU.mult, op1=ALU.add)
+                    nc.vector.tensor_scalar(
+                        out=lines[:, t, :], in0=x, scalar1=number_wb[:, 0, t : t + 1], scalar2=number_wb[:, 1, t : t + 1],
+                        op0=ALU.mult, op1=ALU.add,
+                    )
                 else:
-                    nc.scalar.activation(out=lines[:, t, :], in_=x, func=ACT.Identity, scale=w, bias=b)
+                    nc.scalar.activation(
+                        out=lines[:, t, :], in_=x, func=ACT.Identity,
+                        scale=number_params[:, 0, t : t + 1], bias=number_params[:, 1, t : t + 1],
+                    )
             lines_of[("number", i)] = lines
 
         def tail_lines():
@@ -502,16 +503,16 @@ def tile_claimencoder_kernel(
         take_sine(("head", 2))
         hidden_leaky(0)
         regroup_hidden(1)
-        quantise(("head", 2))
-        layer1(2, False)
         quantise(("hidden", 0))
         layer2_turned(0)
-        regroup_hidden(2)
+        quantise(("head", 2))
+        layer1(2, False)
         prepare_turned()
         lower_out(0)
         hidden_leaky(1)
-        quantise(("hidden", 1))
+        regroup_hidden(2)
         max_out(0)
+        quantise(("hidden", 1))
         layer2_turned(1)
         turn_out(0)
         hidden_leaky(2)

import math
from contextlib import ExitStack

import concourse.mybir as mybir
from concourse.masks import make_identity

F32 = mybir.dt.float32
BF16 = mybir.dt.bfloat16
I32 = mybir.dt.int32
U32 = mybir.dt.uint32
U8 = mybir.dt.uint8
FP8X4 = mybir.dt.float8_e4m3fn_x4
ACT = mybir.ActivationFunctionType
ALU = mybir.AluOpType

P = 128
PACK = 4
K_PASS = P * PACK
CLAIMS = 1536
CHUNK = 512
N_CHUNKS = CLAIMS // CHUNK
QUARTER = 80
POINT_FEATURES = 8 * QUARTER
NUMBER_WIDTH = 128
HIDDEN = 512
OUT_WIDTH = 512
TAIL = POINT_FEATURES - K_PASS
TAIL_PARTITIONS = TAIL // PACK
SLOPE = 0.01
TURN = 2.0 * math.pi

ROW_PHASE = 0
ROW_W = 1
ROW_B = 2
N_ROWS = 3

SRC_X = 0
SRC_Y = 32
DST_X = 64
DST_Y = 96
MARK = 32
B2_ROW = 64

QUADRANTS = P // TAIL_PARTITIONS
TAIL_CLAIMS = CLAIMS // QUADRANTS

FLOPS = 2 * CLAIMS * (2 * K_PASS * HIDDEN + HIDDEN * OUT_WIDTH)


def tile_claimencoder_kernel(
    tc,
    src_xy, dst_xy, time_s, wait_src, wait_dst,
    src_wsx, src_bsx, src_wcx, src_bcx, src_wsy, src_bsy, src_wcy, src_bcy,
    dst_wsx, dst_bsx, dst_wcx, dst_bcx, dst_wsy, dst_bsy, dst_wcy, dst_bcy,
    t_w, t_b, ws_w, ws_b, wd_w, wd_b,
    W1_words, W1_scales, b1, W2_words, W2_scales, b2,
    out,
):
    nc = tc.nc
    with ExitStack() as stack:
        keep = stack.enter_context(tc.tile_pool(name="keep", bufs=1))
        stack.enter_context(tc.manual_schedule())
        work = stack.enter_context(tc.tile_pool(name="work", bufs=3))
        pair = stack.enter_context(tc.tile_pool(name="pair", bufs=2))
        psum = stack.enter_context(tc.psum_pool(name="psum", bufs=8))

        ident = keep.tile([P, P], BF16)
        number_x = keep.tile([P, CLAIMS], BF16)
        number_wb = keep.tile([P, 2, 16], BF16)
        number_params = keep.tile([P, 2, PACK], F32)
        claim_rows = keep.tile([P, 2 * CLAIMS], BF16)
        angle_vecs = keep.tile([P, K_PASS], BF16)
        shift_vecs = keep.tile([P, K_PASS], BF16)
        head_bias = keep.tile([P, PACK], F32)
        ident_f32 = keep.tile([P, P], F32)
        b2_cols = keep.tile([P, OUT_WIDTH // P], F32)
        b2_low = keep.tile([P, OUT_WIDTH // P], F32)
        tail_rows = keep.tile([P, 2 * TAIL_CLAIMS], BF16)
        spread = keep.tile([P, P], BF16)
        tail_vecs = keep.tile([P, K_PASS], BF16)
        b1_cols = keep.tile([P, PACK], BF16)
        phase = keep.tile([P, 1], F32)

        w1_loaded_words = keep.tile([P, 2, HIDDEN], U32, align_bytes=64)
        w1_loaded_scales = keep.tile([P, 2, HIDDEN], U8, align_bytes=64)
        w1_words = keep.tile([P, 2, HIDDEN], U32, align_bytes=64)
        w1_scales = keep.tile([P, 2, HIDDEN], U8, align_bytes=64)
        w2_words = keep.tile([P, OUT_WIDTH], U32, align_bytes=64)
        w2_scales = keep.tile([P, OUT_WIDTH], U8, align_bytes=64)
        b2_all = keep.tile([P, OUT_WIDTH], BF16)

        warm = keep.tile([P, 1], F32)
        nc.vector.memset(warm[:], 0.0)

        for first, count, numbers in ((0, 64, time_s), (64, 32, wait_src), (96, 32, wait_dst)):
            nc.sync.dma_start(out=number_x[first : first + count, :], in_=numbers.partition_broadcast(count))
        for r, (w, b) in enumerate(((t_w, t_b), (ws_w, ws_b), (wd_w, wd_b))):
            rows = slice(32 * (r + 1), 32 * (r + 2))
            nc.scalar.dma_start(out=number_wb[rows, 0, 0:PACK], in_=w.rearrange("(p t) -> p t", t=PACK))
            queue = nc.scalar if r < 2 else nc.gpsimd
            queue.dma_start(out=number_wb[rows, 1, 0:PACK], in_=b.rearrange("(p t) -> p t", t=PACK))
        nc.scalar.activation(out=warm[:], in_=warm[:], func=ACT.Sin)
        nc.gpsimd.memset(w1_loaded_scales[:].bitcast(F32), 0.0)
        nc.gpsimd.memset(w2_scales[:].bitcast(F32), 0.0)
        make_identity(nc, ident[:])
        nc.vector.memset(tail_rows[:], 0.0)
        nc.vector.memset(tail_vecs[:], 0.0)
        nc.vector.memset(number_wb[0:TAIL_PARTITIONS, :, :], 0.0)
        nc.vector.memset(angle_vecs[:], 0.0)
        nc.vector.memset(shift_vecs[:], 0.0)
        parts = shift_vecs[MARK : MARK + 1, 0 : 2 * QUARTER * (K_PASS // (2 * QUARTER))].rearrange(
            "o (h q k) -> o h q k", q=2, k=QUARTER
        )
        nc.vector.memset(parts[:, :, 1, :], 0.25)
        nc.vector.memset(spread[:], 0.0)
        for j in range(QUADRANTS):
            rows = slice(TAIL_PARTITIONS * j, TAIL_PARTITIONS * (j + 1))
            nc.vector.memset(spread[TAIL_PARTITIONS * j : TAIL_PARTITIONS * j + 1, rows], 1.0)

        src_flat = src_xy.rearrange("c two -> (c two)")
        dst_flat = dst_xy.rearrange("c two -> (c two)")
        point_parts = (
            (src_wsx, src_bsx, SRC_X), (src_wcx, src_bcx, SRC_X), (src_wsy, src_bsy, SRC_Y), (src_wcy, src_bcy, SRC_Y),
            (dst_wsx, dst_bsx, DST_X), (dst_wcx, dst_bcx, DST_X), (dst_wsy, dst_bsy, DST_Y), (dst_wcy, dst_bcy, DST_Y),
        )
        nc.sync.dma_start(out=tail_rows[0:P:TAIL_PARTITIONS, :], in_=dst_flat.rearrange("(j e) -> j e", j=QUADRANTS))
        tail_copies = tail_vecs[:].rearrange("p (i k) -> p i k", k=TAIL)
        for q, (w, b, rows) in enumerate(point_parts):
            first = QUARTER * q
            head = max(0, min(QUARTER, K_PASS - first))
            if head < QUARTER:
                rest = QUARTER - head
                at = first + head - K_PASS
                for row, vector in ((ROW_W, w), (ROW_B, b)):
                    nc.sync.dma_start(
                        out=tail_copies[row : row + 1, :, at : at + rest],
                        in_=vector[head:QUARTER].unsqueeze(0).unsqueeze(0).to_broadcast([1, QUADRANTS, rest]),
                    )
                if q % 2 == 1:
                    nc.vector.memset(tail_copies[ROW_PHASE : ROW_PHASE + 1, :, at : at + rest], 0.25)


        for q, (w, b, row) in enumerate(point_parts):
            first = QUARTER * q
            head = max(0, min(QUARTER, K_PASS - first))
            if head > 0:
                nc.sync.dma_start(out=angle_vecs[row : row + 1, first : first + head], in_=w[0:head].unsqueeze(0))
                nc.sync.dma_start(out=shift_vecs[0:1, first : first + head], in_=b[0:head].unsqueeze(0))
        nc.sync.dma_start(out=shift_vecs[B2_ROW : B2_ROW + 1, :], in_=b2.unsqueeze(0))
        for row, flat, shift in ((SRC_X, src_flat, 0), (SRC_Y, src_flat, 1), (DST_X, dst_flat, 0), (DST_Y, dst_flat, 1)):
            nc.sync.dma_start(
                out=claim_rows[row : row + TAIL_PARTITIONS, 0 : 2 * CLAIMS - shift],
                in_=flat[shift : 2 * CLAIMS].partition_broadcast(TAIL_PARTITIONS),
            )
        coordinate = claim_rows[:].rearrange("p (c two) -> p c two", two=2)

        nc.sync.dma_start(
            out=w1_loaded_words[:].bitcast(I32),
            in_=W1_words.rearrange("g p n t -> p g (n t)").bitcast(I32),
        )
        for quad in range(4):
            nc.sync.dma_start(
                out=w1_loaded_scales[32 * quad : 32 * quad + 4, :, :].bitcast(I32),
                in_=W1_scales[:, 4 * quad : 4 * quad + 4, :].rearrange("g r n -> r g n").bitcast(I32),
            )
        nc.sync.dma_start(out=b1_cols[:], in_=b1.rearrange("(p t) -> p t", t=PACK))
        nc.sync.dma_start(
            out=w2_words[:].bitcast(I32),
            in_=W2_words[0].rearrange("p n t -> p (n t)").bitcast(I32),
        )
        for quad in range(4):
            nc.sync.dma_start(
                out=w2_scales[32 * quad : 32 * quad + 4, :].bitcast(I32),
                in_=W2_scales[0, 4 * quad : 4 * quad + 4, :].bitcast(I32),
            )
        nc.sync.dma_start(out=b2_all[:], in_=b2.partition_broadcast(P))

        tail_params = keep.tile([P, PACK, N_ROWS], F32)
        tail_phase = keep.tile([P, 1], F32)
        angles_of = {}
        whole_of = {}
        lines_of = {}
        grouped_of = {}
        codes_of = {}
        scales_of = {}

        def prepare_number():
            nc.scalar.copy(out=number_params[:], in_=number_wb[:, :, 0:PACK])

        def prepare_tail():
            turned = psum.tile([P, PACK, P], BF16, tag="bank")
            for t in range(PACK):
                nc.tensor.transpose(turned[:, t, :], tail_vecs[:, t : K_PASS : PACK], ident[:])
            y_of_tail = psum.tile([P, TAIL_CLAIMS], F32, tag="bank")
            nc.tensor.matmul(
                y_of_tail[:], lhsT=spread[:], rhs=tail_rows[:].rearrange("p (c two) -> p c two", two=2)[:, :, 1],
                start=True, stop=True,
            )
            angles_of["tail"] = y_of_tail
            nc.scalar.copy(out=tail_phase[:], in_=turned[:, 0, ROW_PHASE : ROW_PHASE + 1])
            nc.scalar.mul(out=tail_params[:, :, ROW_W], in_=turned[:, :, ROW_W], mul=1.0 / TURN)
            nc.scalar.activation(
                out=tail_params[:, :, ROW_B], in_=turned[:, :, ROW_B], func=ACT.Identity, scale=1.0 / TURN, bias=tail_phase[:]
            )

        def number_lines(i):
            lines = pair.tile([P, PACK, CHUNK], F32, tag="lines_number")
            for t in range(PACK):
                x = number_x[:, CHUNK * i : CHUNK * (i + 1)]
                if i == 0:
                    nc.vector.tensor_scalar(
                        out=lines[:, t, :], in0=x, scalar1=number_wb[:, 0, t : t + 1], scalar2=number_wb[:, 1, t : t + 1],
                        op0=ALU.mult, op1=ALU.add,
                    )
                else:
                    nc.scalar.activation(
                        out=lines[:, t, :], in_=x, func=ACT.Identity,
                        scale=number_params[:, 0, t : t + 1], bias=number_params[:, 1, t : t + 1],
                    )
            lines_of[("number", i)] = lines

        def tail_lines():
            lines = work.tile([P, PACK, TAIL_CLAIMS], F32, tag="lines")
            for t in range(PACK):
                nc.scalar.activation(
                    out=lines[:, t, :], in_=angles_of["tail"][:], func=ACT.Identity,
                    scale=tail_params[:, t, ROW_W : ROW_W + 1], bias=tail_params[:, t, ROW_B : ROW_B + 1],
                )
            lines_of[("tail", 0)] = lines

        def prepare_head():
            n_tiles = OUT_WIDTH // P
            shifts = psum.tile([P, PACK + 1 + n_tiles], F32, tag="bank")
            for t in range(PACK):
                nc.tensor.matmul(
                    shifts[:, t : t + 1], lhsT=shift_vecs[:, t : K_PASS : PACK], rhs=ident[:, 0:1], start=True, stop=True
                )
            nc.tensor.matmul(
                shifts[:, PACK : PACK + 1], lhsT=shift_vecs[:, 0:K_PASS:PACK], rhs=ident[:, MARK : MARK + 1],
                start=True, stop=True,
            )
            for nt in range(n_tiles):
                nc.tensor.matmul(
                    shifts[:, PACK + 1 + nt : PACK + 2 + nt], lhsT=shift_vecs[:, P * nt : P * (nt + 1)],
                    rhs=ident[:, B2_ROW : B2_ROW + 1], start=True, stop=True,
                )
            nc.scalar.copy(out=phase[:], in_=shifts[:, PACK : PACK + 1])
            nc.scalar.copy(out=b2_cols[:], in_=shifts[:, PACK + 1 : PACK + 1 + n_tiles])
            nc.scalar.activation(
                out=head_bias[:], in_=shifts[:, 0:PACK], func=ACT.Identity, scale=1.0 / TURN, bias=phase[:]
            )

        def head_angles(i):
            angles_of[i] = []
            for t in range(PACK):
                angle = psum.tile([P, CHUNK], F32, tag="bank")
                nc.tensor.matmul(
                    angle[:], lhsT=angle_vecs[:, t : K_PASS : PACK], rhs=coordinate[:, CHUNK * i : CHUNK * (i + 1), 0],
                    start=True, stop=True,
                )
                angles_of[i].append(angle)

        def head_lines(i):
            lines = work.tile([P, PACK, CHUNK], F32, tag="lines")
            for t in range(PACK):
                nc.scalar.activation(
                    out=lines[:, t, :], in_=angles_of[i][t][:], func=ACT.Identity, scale=1.0 / TURN,
                    bias=head_bias[:, t : t + 1],
                )
            lines_of[("head", i)] = lines

        def leaky_grouped(lines, grouped):
            by_claim = lines[:].rearrange("p t c -> p c t")
            nc.vector.scalar_tensor_tensor(
                out=grouped[:], in0=by_claim, scalar=SLOPE, in1=by_claim, op0=ALU.mult, op1=ALU.max
            )

        def number_leaky(i):
            grouped = work.tile([P, CHUNK, PACK], BF16, align_bytes=64, tag="grouped_number")
            leaky_grouped(lines_of[("number", i)], grouped)
            grouped_of[("number", i)] = grouped

        def width_of(unit):
            return TAIL_CLAIMS if unit[0] == "tail" else CHUNK

        def move_tail(i):
            for j in range(QUADRANTS):
                first = max(CHUNK * i, TAIL_CLAIMS * j)
                last = min(CHUNK * (i + 1), TAIL_CLAIMS * (j + 1))
                if first < last:
                    nc.sync.dma_start(
                        out=grouped_of[("number", i)][0:TAIL_PARTITIONS, first - CHUNK * i : last - CHUNK * i, :],
                        in_=grouped_of[TAIL_UNIT][
                            TAIL_PARTITIONS * j : TAIL_PARTITIONS * (j + 1), first - TAIL_CLAIMS * j : last - TAIL_CLAIMS * j, :
                        ],
                    )

        def whole_turns(unit):
            whole = pair.tile([P, PACK, width_of(unit)], I32)
            nc.vector.tensor_copy(out=whole[:], in_=lines_of[unit][:])
            whole_of[unit] = whole

        def drop_turns(unit):
            lines = lines_of[unit]
            nc.vector.tensor_tensor(out=lines[:], in0=lines[:], in1=whole_of[unit][:], op=ALU.subtract)

        def take_sine(unit):
            grouped = work.tile([P, width_of(unit), PACK], BF16, align_bytes=64)
            nc.scalar.activation(
                out=grouped[:].rearrange("p (c i) t -> p c t i", i=4),
                in_=lines_of[unit][:].rearrange("p t (c i) -> p c t i", i=4),
                func=ACT.Sin, scale=TURN,
            )
            grouped_of[unit] = grouped

        def quantise(unit):
            codes = keep.tile([P, CHUNK], U32, align_bytes=64, name="codes_%s%d" % unit)
            scales = keep.tile([P, CHUNK], U8, align_bytes=64, name="scales_%s%d" % unit)
            nc.vector.quantize_mx(
                out=codes[:].bitcast(FP8X4), scales=scales[:], in_=grouped_of[unit][:].rearrange("p c t -> p (c t)")
            )
            codes_of[unit] = codes
            scales_of[unit] = scales

        sums_of = {}

        def permute_w1():
            nc.vector.tensor_copy(
                out=w1_words[:].bitcast(I32).rearrange("p g (t m) -> p g t m", t=PACK),
                in_=w1_loaded_words[:].bitcast(I32).rearrange("p g (m t) -> p g t m", t=PACK),
            )
            nc.vector.tensor_copy(
                out=w1_scales[:].rearrange("p g (t m) -> p g t m", t=PACK),
                in_=w1_loaded_scales[:].rearrange("p g (m t) -> p g t m", t=PACK),
            )

        def layer1(i, opening):
            if opening:
                sums_of[i] = [psum.tile([P, CHUNK], F32, tag="bank", name="acc%d_%d" % (i, mt)) for mt in range(HIDDEN // P)]
            g, unit = (1, ("number", i)) if opening else (0, ("head", i))
            for mt in range(HIDDEN // P):
                units_mt = slice(P * mt, P * (mt + 1))
                nc.tensor.matmul_mx(
                    out=sums_of[i][mt][:],
                    lhsT=w1_words[:, g, units_mt].bitcast(FP8X4),
                    lhsT_scale=w1_scales[:, g, units_mt],
                    rhs=codes_of[unit][:].bitcast(FP8X4),
                    rhs_scale=scales_of[unit][:],
                    start=opening,
                    stop=not opening,
                )

        def regroup_hidden(i):
            regrouped = pair.tile([P, PACK, CHUNK], F32)
            for t in range(PACK):
                nc.scalar.activation(
                    out=regrouped[:, t, :], in_=sums_of[i][t][:], func=ACT.Identity, bias=b1_cols[:, t : t + 1], scale=1.0
                )
            lines_of[("hidden", i)] = regrouped

        def hidden_leaky(i):
            h = pair.tile([P, CHUNK, PACK], BF16, align_bytes=64)
            leaky_grouped(lines_of[("hidden", i)], h)
            grouped_of[("hidden", i)] = h

        def layer2(i):
            codes, scales = codes_of[("hidden", i)], scales_of[("hidden", i)]
            sums_of[("layer2", i)] = []
            for j in range(CHUNK // P):
                claims = slice(P * j, P * (j + 1))
                acc = psum.tile([P, OUT_WIDTH], F32, tag="bank")
                nc.tensor.matmul_mx(
                    out=acc[:],
                    lhsT=codes[:, claims].bitcast(FP8X4),
                    lhsT_scale=scales[:, claims],
                    rhs=w2_words[:].bitcast(FP8X4),
                    rhs_scale=w2_scales[:],
                    start=True,
                    stop=True,
                )
                sums_of[("layer2", i)].append(acc)

        def prepare_turned():
            nc.scalar.copy(out=ident_f32[:], in_=ident[:])
            nc.scalar.mul(out=b2_low[:], in_=b2_cols[:], mul=SLOPE)

        def layer2_turned(i):
            codes, scales = codes_of[("hidden", i)], scales_of[("hidden", i)]
            sums_of[("layer2", i)] = []
            for nt in range(OUT_WIDTH // P):
                channels = slice(P * nt, P * (nt + 1))
                acc = psum.tile([P, CHUNK], F32, tag="bank")
                nc.tensor.matmul_mx(
                    out=acc[:],
                    lhsT=w2_words[:, channels].bitcast(FP8X4),
                    lhsT_scale=w2_scales[:, channels],
                    rhs=codes[:].bitcast(FP8X4),
                    rhs_scale=scales[:],
                    start=True,
                    stop=True,
                )
                sums_of[("layer2", i)].append(acc)

        def lower_out(i):
            low = pair.tile([P, OUT_WIDTH // P, CHUNK], F32, tag="z")
            for nt in range(OUT_WIDTH // P):
                nc.scalar.activation(
                    out=low[:, nt, :], in_=sums_of[("layer2", i)][nt][:], func=ACT.Identity, scale=SLOPE,
                    bias=b2_low[:, nt : nt + 1],
                )
            sums_of[("low", i)] = low

        def max_out(i):
            channels_first = pair.tile([P, OUT_WIDTH // P, CHUNK], F32)
            for nt in range(OUT_WIDTH // P):
                nc.vector.scalar_tensor_tensor(
                    out=channels_first[:, nt, :], in0=sums_of[("layer2", i)][nt][:], scalar=b2_cols[:, nt : nt + 1],
                    in1=sums_of[("low", i)][:, nt, :], op0=ALU.add, op1=ALU.max,
                )
            sums_of[("out", i)] = channels_first

        def turn_out(i):
            sums_of[("turned", i)] = []
            for j in range(CHUNK // P):
                bank = psum.tile([P, OUT_WIDTH], F32, tag="bank")
                for nt in range(OUT_WIDTH // P):
                    nc.tensor.transpose(
                        bank[:, P * nt : P * (nt + 1)], sums_of[("out", i)][:, nt, P * j : P * (j + 1)], ident_f32[:]
                    )
                sums_of[("turned", i)].append(bank)

        def store_turned(i):
            claims_first = pair.tile([P, CHUNK // P, OUT_WIDTH], F32)
            for j in range(CHUNK // P):
                nc.scalar.copy(out=claims_first[:, j, :], in_=sums_of[("turned", i)][j][:])
                first = CHUNK * i + P * j
                nc.sync.dma_start(out=out[first : first + P, :], in_=claims_first[:, j, :])

        def add_b2(i):
            z = pair.tile([P, CHUNK // P, OUT_WIDTH], F32, tag="z")
            for j in range(CHUNK // P):
                nc.vector.tensor_tensor(out=z[:, j, :], in0=sums_of[("layer2", i)][j][:], in1=b2_all[:], op=ALU.add)
            sums_of[("out", i)] = z

        def finish_out(i):
            z = sums_of[("out", i)]
            result = pair.tile([P, CHUNK // P, OUT_WIDTH], F32)
            pieces = CHUNK // P if i == N_CHUNKS - 1 else 1
            tiles = CHUNK // P // pieces
            for n in range(pieces):
                js = slice(tiles * n, tiles * (n + 1))
                nc.vector.scalar_tensor_tensor(
                    out=result[:, js, :], in0=z[:, js, :], scalar=SLOPE, in1=z[:, js, :], op0=ALU.mult, op1=ALU.max
                )
                first = CHUNK * i + P * tiles * n
                nc.sync.dma_start(
                    out=out[first : first + P * tiles, :].rearrange("(j p) n -> p j n", p=P), in_=result[:, js, :]
                )

        TAIL_UNIT = ("tail", 0)
        prepare_number()
        number_lines(0)
        number_lines(1)
        number_leaky(0)
        prepare_tail()
        tail_lines()
        number_leaky(1)
        number_lines(2)
        whole_turns(TAIL_UNIT)
        prepare_head()
        head_angles(0)
        head_lines(0)
        drop_turns(TAIL_UNIT)
        number_leaky(2)
        head_angles(1)
        take_sine(TAIL_UNIT)
        move_tail(0)
        move_tail(1)
        move_tail(2)
        whole_turns(("head", 0))
        head_lines(1)
        head_angles(2)
        drop_turns(("head", 0))
        permute_w1()
        take_sine(("head", 0))
        whole_turns(("head", 1))
        quantise(("number", 0))
        layer1(0, True)
        drop_turns(("head", 1))
        head_lines(2)
        quantise(("number", 1))
        quantise(("head", 0))
        layer1(0, False)
        layer1(1, True)
        take_sine(("head", 1))
        whole_turns(("head", 2))
        regroup_hidden(0)
        quantise(("number", 2))
        drop_turns(("head", 2))
        quantise(("head", 1))
        layer1(1, False)
        layer1(2, True)
        take_sine(("head", 2))
        hidden_leaky(0)
        regroup_hidden(1)
        quantise(("hidden", 0))
        layer2_turned(0)
        quantise(("head", 2))
        layer1(2, False)
        prepare_turned()
        lower_out(0)
        hidden_leaky(1)
        regroup_hidden(2)
        max_out(0)
        quantise(("hidden", 1))
        layer2_turned(1)
        turn_out(0)
        hidden_leaky(2)
        lower_out(1)
        store_turned(0)
        quantise(("hidden", 2))
        max_out(1)
        layer2(2)
        turn_out(1)
        add_b2(2)
        store_turned(1)
        finish_out(2)
